import numpy as np
import ml_dtypes


def mxq(x, axis, fmt="e4m3"):
    dtype, down = {"e4m3": (ml_dtypes.float8_e4m3fn, 7), "e5m2": (ml_dtypes.float8_e5m2, 14)}[fmt]
    v = np.moveaxis(np.asarray(x, np.float32).astype(ml_dtypes.bfloat16).astype(np.float64), axis, -1)
    blocks = v.reshape(v.shape[:-1] + (-1, 32))
    amax = np.abs(blocks).max(-1, keepdims=True)
    byte = np.maximum(np.where(amax > 0, np.frexp(amax)[1] - 1 + 127, 0) - down, 1)
    scale = np.exp2(byte - 127.0)
    codes = (blocks / scale).astype(np.float32).astype(dtype).astype(np.float64)
    return np.moveaxis((codes * scale).reshape(v.shape), -1, axis)


WIDE = False


def mx_kscale(k):
    if not WIDE:
        return np.ones(k)
    levels = np.array([10, -10, 5, -5, 0])
    a = np.random.permutation(np.resize(levels, k // 512 * 4)).reshape(k // 512, 4)
    idx = np.arange(k)
    return np.exp2(a[idx // 512, idx % 128 // 32])


BF16 = ml_dtypes.bfloat16


def bf(x):
    return np.asarray(x, np.float32).astype(BF16)


def f64(x):
    return np.asarray(x).astype(np.float64)


E2M1 = np.array([0.0, 0.5, 1.0, 1.5, 2.0, 3.0, 4.0, 6.0, -0.0, -0.5, -1.0, -1.5, -2.0, -3.0, -4.0, -6.0])


def pack_weight(w, fmt):
    k, n = w.shape
    w = f64(bf(w)).reshape(k // 32, 32, n)
    amax = np.abs(w).max(1)
    if fmt == "e4m3":
        byte = np.frexp(amax)[1] - 1 + 127 - 7
    else:
        mant, ex = np.frexp(amax / 6.0)
        byte = np.where(mant > 0.5, ex, ex - 1) + 127
    byte = np.clip(np.where(amax > 0, byte, 1), 1, 254)
    scaled = (w * np.exp2(127.0 - byte)[:, None, :]).reshape(k, n).astype(np.float32)
    by_word = np.ascontiguousarray(scaled.reshape(k // 512, 128, 4, n).transpose(0, 1, 3, 2))
    if fmt == "e4m3":
        words = by_word.astype(ml_dtypes.float8_e4m3fn).view(np.uint8)
    else:
        c = by_word.astype(ml_dtypes.float4_e2m1fn).view(np.uint8) & 0xF
        words = c[..., 0::2] | (c[..., 1::2] << 4)
    return np.ascontiguousarray(words), np.ascontiguousarray(byte.astype(np.uint8).reshape(k // 512, 16, n))


def unpack_weight(words, scales, fmt):
    g, p, n, _ = words.shape
    if fmt == "e4m3":
        vals = np.ascontiguousarray(words).view(ml_dtypes.float8_e4m3fn).astype(np.float64)
    else:
        nib = np.empty((g, p, n, 4), np.uint8)
        nib[..., 0::2] = words & 0xF
        nib[..., 1::2] = words >> 4
        vals = E2M1[nib]
    vals = vals * np.repeat(np.exp2(scales.astype(np.float64) - 127.0), 8, axis=1)[..., None]
    return vals.transpose(0, 1, 3, 2).reshape(g * 512, n)

def pack4(w):
    words, scales = pack_weight(w, "e2m1")
    return words.reshape(words.shape[0], 128, -1), scales


def unpack4(words, scales):
    return unpack_weight(words.reshape(words.shape[0], 128, -1, 2), scales, "e2m1")


B, K, N = 1024, 1024, 1024


def setup_inputs():
    s = mx_kscale(K)
    s = s / s.max()
    x = bf(np.random.standard_normal((B, K)) * s)
    W_words, W_scales = pack4(np.random.standard_normal((K, N)) * 0.4 / np.sqrt(K) / s[:, None])
    return {"x": x,
            "W_words": W_words,
            "W_scales": W_scales,
            "P": bf(np.random.standard_normal(N) * 0.3),
            "w": bf(0.8 + 0.1 * np.random.standard_normal(1)),
            "p": bf(0.5 + 0.1 * np.random.standard_normal(1)),
            "sine_w": bf(1.2 + 0.1 * np.random.standard_normal(1)),
            "cosine_w": bf(-0.7 + 0.1 * np.random.standard_normal(1))}


def reference(x, W_words, W_scales, P, w, p, sine_w, cosine_w):
    x = f64(x)
    original = f64(w) * x + f64(p)
    z = (mxq(x, 1, "e4m3") @ unpack4(W_words, W_scales)) + f64(P)
    periodic = f64(sine_w) * np.sin(z) + f64(cosine_w) * np.cos(z)
    return np.concatenate((original, periodic), axis=-1)

@@ -1,0 +1,329 @@
+import math
+from contextlib import ExitStack
+
+import concourse.mybir as mybir
+from concourse.masks import make_identity
+
+F32 = mybir.dt.float32
+BF16 = mybir.dt.bfloat16
+I32 = mybir.dt.int32
+U32 = mybir.dt.uint32
+U8 = mybir.dt.uint8
+FP8X4 = mybir.dt.float8_e4m3fn_x4
+FP4X4 = mybir.dt.float4_e2m1fn_x4
+ALU = mybir.AluOpType
+ACT = mybir.ActivationFunctionType
+
+P = 128
+PACK = 4
+BATCH, K_DIM, N_DIM = 1024, 1024, 1024
+PASSES = K_DIM // (P * PACK)
+BANK = 512
+ROW_TILES = BATCH // P
+N_TILES = N_DIM // P
+PER_BANK = BANK // P
+HALVES = BATCH // BANK
+UNITS = HALVES * (N_TILES // PER_BANK)
+
+TWO_PI = 2.0 * math.pi
+HALF_PI = 0.5 * math.pi
+TINY = 1e-30
+SLOTS = UNITS * PER_BANK
+
+FLOPS = 2 * BATCH * K_DIM * N_DIM
+
+
+def tile_time2vec_kernel(tc, x, W_words, W_scales, P_vec, w, p, sine_w, cosine_w, out):
+    nc = tc.nc
+    with ExitStack() as ctx:
+        ctx.enter_context(tc.manual_schedule())
+        keep = ctx.enter_context(tc.tile_pool(name="keep", bufs=1))
+        tiny = ctx.enter_context(tc.tile_pool(name="tiny", bufs=1))
+        work = ctx.enter_context(tc.tile_pool(name="work", bufs=4))
+        waves = ctx.enter_context(tc.tile_pool(name="waves", bufs=2))
+        leaving = ctx.enter_context(tc.tile_pool(name="leaving", bufs=8))
+        psum_z = ctx.enter_context(tc.psum_pool(name="psum_z", bufs=PER_BANK))
+        psum_t = ctx.enter_context(tc.psum_pool(name="psum_t", bufs=PER_BANK))
+
+        sine_bf = tiny.tile([P, 1], BF16)
+        nc.sync.dma_start(out=sine_bf[:], in_=sine_w.partition_broadcast(P))
+        cosine_bf = tiny.tile([P, 1], BF16)
+        nc.sync.dma_start(out=cosine_bf[:], in_=cosine_w.partition_broadcast(P))
+        p_rows_bf = keep.tile([P, P], BF16)
+        nc.vector.memset(p_rows_bf[:], 0.0)
+        nc.scalar.dma_start(out=p_rows_bf[0:N_TILES, :], in_=P_vec.rearrange("(j n) -> j n", n=P))
+        zero = tiny.tile([P, 1], F32)
+        nc.vector.memset(zero[:], 0.0)
+        warm = tiny.tile([P, 1], F32)
+        nc.scalar.activation(out=warm[:], in_=zero[:], func=ACT.Sin)
+
+        w_scales = keep.tile([P, PASSES, N_DIM], U8, align_bytes=64)
+        nc.vector.memset(w_scales[:].bitcast(I32), 0)
+        scale_rows = W_scales.bitcast(I32).rearrange("g (quad r) n -> r quad g n", r=4)
+        x_sb = keep.tile([P, ROW_TILES, K_DIM], BF16)
+        x_rows = x.rearrange("(i b) k -> i b k", b=P)
+        w_words = keep.tile([P, PASSES, 2 * N_DIM], U8, align_bytes=64)
+        w_bf = tiny.tile([P, 1], BF16)
+        p_bf = tiny.tile([P, 1], BF16)
+
+        for i in range(PER_BANK):
+            nc.sync.dma_start(out=x_sb[:, i, :], in_=x_rows[i])
+        for r in range(4):
+            nc.sync.dma_start(out=w_scales[r:P:32, :, :].bitcast(I32), in_=scale_rows[r])
+        nc.sync.dma_start(out=w_words[:].bitcast(I32), in_=W_words.bitcast(I32).rearrange("g p n -> p g n"))
+        nc.sync.dma_start(out=w_bf[:], in_=w.partition_broadcast(P))
+        nc.sync.dma_start(out=p_bf[:], in_=p.partition_broadcast(P))
+        for i in range(PER_BANK, ROW_TILES):
+            nc.sync.dma_start(out=x_sb[:, i, :], in_=x_rows[i])
+
+        ident = keep.tile([P, P], F32)
+        make_identity(nc, ident[:])
+        one_half = tiny.tile([P, 1], F32)
+        nc.gpsimd.memset(one_half[:], 0.5)
+
+        grouped = keep.tile([P, HALVES, PASSES, BANK, PACK], BF16, align_bytes=64)
+        x_codes = keep.tile([P, HALVES, PASSES, BANK], U32, align_bytes=64)
+        x_scales = keep.tile([P, HALVES, PASSES, BANK], U8, align_bytes=64)
+
+        def turn_rows(i):
+            words = x_sb[:, i, :].bitcast(F32)
+            turned = psum_t.tile([P, PASSES, 2, P], F32, tag="turned")
+            for g in range(PASSES):
+                for u in range(2):
+                    nc.tensor.transpose(
+                        out=turned[:, g, u, :], in_=words[:, 256 * g + u : 256 * (g + 1) : 2], identity=ident[:]
+                    )
+            return turned
+
+        def regroup(i, turned):
+            half, c = divmod(i, PER_BANK)
+            nc.scalar.copy(
+                out=grouped[:, half, :, c * P : (c + 1) * P, :].bitcast(F32),
+                in_=turned[:].rearrange("p g u b -> p g b u"),
+            )
+
+        def quantise_tile(i, g):
+            half, c = divmod(i, PER_BANK)
+            cols = slice(c * P, (c + 1) * P)
+            nc.vector.quantize_mx(
+                out=x_codes[:, half, g, cols].bitcast(FP8X4),
+                scales=x_scales[:, half, g, cols],
+                in_=grouped[:, half, g, cols, :].rearrange("p b t -> p (b t)"),
+            )
+
+        def quantise_half(half):
+            nc.vector.quantize_mx(
+                out=x_codes[:, half, :, :].rearrange("p g b -> p (g b)").bitcast(FP8X4),
+                scales=x_scales[:, half, :, :].rearrange("p g b -> p (g b)"),
+                in_=grouped[:, half, :, :, :].rearrange("p g b t -> p (g b t)"),
+            )
+
+        def place(slot):
+            unit_no, position = divmod(slot, PER_BANK)
+            half, group = divmod(unit_no, N_TILES // PER_BANK)
+            return half, group, position
+
+        def multiply(slot):
+            half, group, position = place(slot)
+            j = group * PER_BANK + position
+            z_t = psum_z.tile([P, BANK], F32)
+            for g in range(PASSES):
+                nc.tensor.matmul_mx(
+                    out=z_t[:],
+                    lhsT=w_words[:, g, 2 * P * j : 2 * P * (j + 1)].bitcast(FP4X4),
+                    lhsT_scale=w_scales[:, g, P * j : P * (j + 1)],
+                    rhs=x_codes[:, half, g, :].bitcast(FP8X4),
+                    rhs_scale=x_scales[:, half, g, :],
+                    start=(g == 0),
+                    stop=(g == PASSES - 1),
+                )
+            return z_t
+
+        def nearest(slot, z_t):
+            half, group, position = place(slot)
+            j = group * PER_BANK + position
+            whole = work.tile([P, BANK], I32)
+            nc.vector.tensor_scalar(
+                out=whole[:], in0=z_t[:], scalar1=1.0 / TWO_PI, scalar2=bias_turns[:, j : j + 1],
+                op0=ALU.mult, op1=ALU.add,
+            )
+            return whole
+
+        def sine(slot, z_t, whole, wave):
+            half, group, position = place(slot)
+            j = group * PER_BANK + position
+            frac = work.tile([P, BANK], F32)
+            nc.vector.scalar_tensor_tensor(
+                out=frac[:], in0=z_t[:], scalar=1.0 / TWO_PI, in1=whole[:], op0=ALU.mult, op1=ALU.subtract
+            )
+            nc.scalar.activation(
+                out=wave[:, position, :], in_=frac[:], func=ACT.Sin, scale=TWO_PI, bias=bias_rad[:, j : j + 1]
+            )
+
+        def turn_back(c, wave):
+            back = psum_t.tile([P, BANK], F32, tag="turned")
+            for position in range(PER_BANK):
+                nc.tensor.transpose(
+                    out=back[:, position * P : (position + 1) * P],
+                    in_=wave[:, position, c * P : (c + 1) * P],
+                    identity=ident[:],
+                )
+            return back
+
+        def leave(slot, back):
+            half, group, c = place(slot)
+            periodic = leaving.tile([P, BANK], F32)
+            if slot >= SLOTS - PER_BANK and c % 2 == 1:
+                nc.vector.tensor_scalar(out=periodic[:], in0=back[:], scalar1=amp[:, 0:1], scalar2=None, op0=ALU.mult)
+            else:
+                nc.scalar.activation(out=periodic[:], in_=back[:], func=ACT.Copy, scale=amp[:, 0:1])
+            rows = slice((half * PER_BANK + c) * P, (half * PER_BANK + c + 1) * P)
+            nc.sync.dma_start(out=out[rows, K_DIM + group * BANK : K_DIM + (group + 1) * BANK], in_=periodic[:])
+
+        def linear(i):
+            original = leaving.tile([P, K_DIM], F32)
+            nc.gpsimd.tensor_scalar(
+                out=original[:], in0=x_sb[:, i, :], scalar1=w32[:, 0:1], scalar2=p32[:, 0:1], op0=ALU.mult, op1=ALU.add
+            )
+            nc.sync.dma_start(out=out[i * P : (i + 1) * P, 0:K_DIM], in_=original[:])
+
+        abs_sine = tiny.tile([P, 1], F32)
+        nc.vector.scalar_tensor_tensor(
+            out=abs_sine[:], in0=sine_bf[:], scalar=-1.0, in1=sine_bf[:], op0=ALU.mult, op1=ALU.max
+        )
+        abs_cosine = tiny.tile([P, 1], F32)
+        nc.vector.scalar_tensor_tensor(
+            out=abs_cosine[:], in0=cosine_bf[:], scalar=-1.0, in1=cosine_bf[:], op0=ALU.mult, op1=ALU.max
+        )
+        twice = tiny.tile([P, 1], F32)
+        nc.vector.tensor_scalar(out=twice[:], in0=cosine_bf[:], scalar1=0.0, scalar2=2.0, op0=ALU.is_ge, op1=ALU.mult)
+        size = tiny.tile([P, 1], F32)
+        nc.vector.scalar_tensor_tensor(
+            out=size[:], in0=abs_cosine[:], scalar=TINY, in1=abs_sine[:], op0=ALU.max, op1=ALU.add
+        )
+        quarter = tiny.tile([P, 1], F32)
+        nc.vector.tensor_scalar(out=quarter[:], in0=twice[:], scalar1=1.0, scalar2=HALF_PI, op0=ALU.subtract, op1=ALU.mult)
+        inv_size = tiny.tile([P, 1], F32)
+        nc.vector.reciprocal(out=inv_size[:], in_=size[:])
+        neg_quarter = tiny.tile([P, 1], F32)
+        nc.vector.tensor_scalar(out=neg_quarter[:], in0=quarter[:], scalar1=-1.0, scalar2=None, op0=ALU.mult)
+        sign = tiny.tile([P, 1], F32)
+        nc.vector.tensor_scalar(out=sign[:], in0=twice[:], scalar1=1.0, scalar2=None, op0=ALU.subtract)
+        unit = tiny.tile([P, 2], F32)
+        nc.vector.tensor_tensor(out=unit[:, 0:1], in0=sine_bf[:], in1=inv_size[:], op=ALU.mult)
+        abs_second = tiny.tile([P, 1], F32)
+        nc.vector.scalar_tensor_tensor(
+            out=abs_second[:], in0=abs_cosine[:], scalar=TINY, in1=inv_size[:], op0=ALU.max, op1=ALU.mult
+        )
+        regroup(0, turn_rows(0))
+        angles = tiny.tile([P, 2], F32)
+        nc.vector.tensor_scalar(
+            out=angles[:, 0:1], in0=unit[:, 0:1], scalar1=neg_quarter[:, 0:1], scalar2=quarter[:, 0:1],
+            op0=ALU.mult, op1=ALU.add,
+        )
+        nc.vector.tensor_scalar(out=angles[:, 1:2], in0=unit[:, 0:1], scalar1=HALF_PI, scalar2=None, op0=ALU.mult)
+        sin_cos = tiny.tile([P, 2], F32)
+        nc.scalar.activation(out=sin_cos[:], in_=angles[:], func=ACT.Sin)
+        nc.vector.tensor_tensor(out=unit[:, 1:2], in0=abs_second[:], in1=sign[:], op=ALU.mult)
+        neg_first = tiny.tile([P, 1], F32)
+        nc.vector.tensor_scalar(out=neg_first[:], in0=unit[:, 0:1], scalar1=-1.0, scalar2=None, op0=ALU.mult)
+        p_rows = keep.tile([P, P], F32)
+        nc.gpsimd.tensor_copy(out=p_rows[:], in_=p_rows_bf[:])
+        squares = tiny.tile([P, 2], F32)
+        nc.gpsimd.tensor_tensor(out=squares[:], in0=unit[:], in1=unit[:], op=ALU.mult)
+        norm2 = tiny.tile([P, 1], F32)
+        nc.gpsimd.tensor_tensor(out=norm2[:], in0=squares[:, 0:1], in1=squares[:, 1:2], op=ALU.add)
+        norm = tiny.tile([P, 1], F32)
+        nc.gpsimd.tensor_tensor(out=norm[:], in0=norm2[:], in1=one_half[:], op=ALU.pow)
+        amp = tiny.tile([P, 1], F32)
+        nc.gpsimd.tensor_tensor(out=amp[:], in0=size[:], in1=norm[:], op=ALU.mult)
+
+        regroup(1, turn_rows(1))
+        p_turned = psum_t.tile([P, P], F32, tag="turned")
+        nc.tensor.transpose(out=p_turned[:], in_=p_rows[:], identity=ident[:])
+        regroup(2, turn_rows(2))
+        regroup(3, turn_rows(3))
+
+        quantise_tile(0, 0)
+        quantise_tile(0, 1)
+        by_cos = tiny.tile([P, 2], F32)
+        nc.vector.tensor_scalar(out=by_cos[:], in0=unit[:], scalar1=sin_cos[:, 1:2], scalar2=None, op0=ALU.mult)
+        p_cols = tiny.tile([P, N_TILES], F32)
+        nc.vector.tensor_copy(out=p_cols[:], in_=p_turned[:, 0:N_TILES])
+        cross = tiny.tile([P, 1], F32)
+        nc.vector.scalar_tensor_tensor(
+            out=cross[:], in0=sin_cos[:, 0:1], scalar=neg_first[:, 0:1], in1=by_cos[:, 1:2], op0=ALU.mult, op1=ALU.add
+        )
+        dot = tiny.tile([P, 1], F32)
+        nc.vector.scalar_tensor_tensor(
+            out=dot[:], in0=sin_cos[:, 0:1], scalar=unit[:, 1:2], in1=by_cos[:, 0:1], op0=ALU.mult, op1=ALU.add
+        )
+        quantise_tile(1, 0)
+        inv_dot = tiny.tile([P, 1], F32)
+        nc.vector.reciprocal(out=inv_dot[:], in_=dot[:])
+        quantise_tile(1, 1)
+        slope = tiny.tile([P, 1], F32)
+        nc.vector.tensor_tensor(out=slope[:], in0=cross[:], in1=inv_dot[:], op=ALU.mult)
+        quantise_tile(2, 0)
+        slope2 = tiny.tile([P, 1], F32)
+        nc.vector.tensor_tensor(out=slope2[:], in0=slope[:], in1=slope[:], op=ALU.mult)
+        quantise_tile(2, 1)
+        low = tiny.tile([P, 1], F32)
+        nc.vector.tensor_scalar(out=low[:], in0=slope2[:], scalar1=-1.0 / 3.0, scalar2=1.0, op0=ALU.mult, op1=ALU.add)
+        high = tiny.tile([P, 1], F32)
+        nc.vector.tensor_scalar(
+            out=high[:], in0=slope2[:], scalar1=-1.0 / 7.0, scalar2=1.0 / 5.0, op0=ALU.mult, op1=ALU.add
+        )
+        slope4 = tiny.tile([P, 1], F32)
+        nc.vector.tensor_tensor(out=slope4[:], in0=slope2[:], in1=slope2[:], op=ALU.mult)
+        quantise_tile(3, 0)
+        series = tiny.tile([P, 1], F32)
+        nc.vector.scalar_tensor_tensor(
+            out=series[:], in0=high[:], scalar=slope4[:, 0:1], in1=low[:], op0=ALU.mult, op1=ALU.add
+        )
+        quantise_tile(3, 1)
+        phase = tiny.tile([P, 1], F32)
+        nc.vector.tensor_scalar(
+            out=phase[:], in0=series[:], scalar1=slope[:, 0:1], scalar2=angles[:, 0:1], op0=ALU.mult, op1=ALU.add
+        )
+        bias_turns = tiny.tile([P, N_TILES], F32)
+        nc.vector.tensor_scalar(
+            out=bias_turns[:], in0=p_cols[:], scalar1=phase[:, 0:1], scalar2=1.0 / TWO_PI, op0=ALU.add, op1=ALU.mult
+        )
+        bias_rad = tiny.tile([P, N_TILES], F32)
+        nc.gpsimd.tensor_scalar(out=bias_rad[:], in0=p_cols[:], scalar1=phase[:, 0:1], scalar2=None, op0=ALU.add)
+        w32 = tiny.tile([P, 1], F32)
+        nc.gpsimd.tensor_copy(out=w32[:], in_=w_bf[:])
+        p32 = tiny.tile([P, 1], F32)
+        nc.gpsimd.tensor_copy(out=p32[:], in_=p_bf[:])
+
+        z_tiles = {}
+        for slot in range(PER_BANK):
+            z_tiles[slot] = multiply(slot)
+        late_rows = {}
+        for i in range(PER_BANK, ROW_TILES):
+            late_rows[i] = turn_rows(i)
+
+        wholes = {0: nearest(0, z_tiles[0])}
+        backs = {}
+        wave = None
+        for slot in range(SLOTS + PER_BANK):
+            if slot + 1 < SLOTS:
+                wholes[slot + 1] = nearest(slot + 1, z_tiles[slot + 1])
+            if slot < SLOTS:
+                if slot % PER_BANK == 0:
+                    wave = waves.tile([P, PER_BANK, BANK], F32, name="wave")
+                sine(slot, z_tiles[slot], wholes[slot], wave)
+            if slot < ROW_TILES - PER_BANK:
+                regroup(PER_BANK + slot, late_rows[PER_BANK + slot])
+            if slot == ROW_TILES - PER_BANK:
+                quantise_half(1)
+            if slot >= PER_BANK:
+                leave(slot - PER_BANK, backs[slot - PER_BANK])
+            if slot + PER_BANK < SLOTS:
+                z_tiles[slot + PER_BANK] = multiply(slot + PER_BANK)
+            if slot < ROW_TILES:
+                linear(slot)
+            if slot < SLOTS and slot % PER_BANK == PER_BANK - 1:
+                for c in range(PER_BANK):
+                    backs[slot - (PER_BANK - 1) + c] = turn_back(c, wave)

@@ -36,7 +36,6 @@ FLOPS = 2 * BATCH * K_DIM * N_DIM
 def tile_time2vec_kernel(tc, x, W_words, W_scales, P_vec, w, p, sine_w, cosine_w, out):
     nc = tc.nc
     with ExitStack() as ctx:
-        ctx.enter_context(tc.manual_schedule())
         keep = ctx.enter_context(tc.tile_pool(name="keep", bufs=1))
         tiny = ctx.enter_context(tc.tile_pool(name="tiny", bufs=1))
         work = ctx.enter_context(tc.tile_pool(name="work", bufs=4))

@@ -181,7 +181,7 @@ def tile_time2vec_kernel(tc, x, W_words, W_scales, P_vec, w, p, sine_w, cosine_w
 
         def linear(i):
             original = leaving.tile([P, K_DIM], F32)
-            nc.gpsimd.tensor_scalar(
+            nc.vector.tensor_scalar(
                 out=original[:], in0=x_sb[:, i, :], scalar1=w32[:, 0:1], scalar2=p32[:, 0:1], op0=ALU.mult, op1=ALU.add
             )
             nc.sync.dma_start(out=out[i * P : (i + 1) * P, 0:K_DIM], in_=original[:])

@@ -27,6 +27,7 @@ UNITS = HALVES * (N_TILES // PER_BANK)
 
 TWO_PI = 2.0 * math.pi
 HALF_PI = 0.5 * math.pi
+APART = 16
 TINY = 1e-30
 SLOTS = UNITS * PER_BANK
 
@@ -44,10 +45,14 @@ def tile_time2vec_kernel(tc, x, W_words, W_scales, P_vec, w, p, sine_w, cosine_w
         psum_z = ctx.enter_context(tc.psum_pool(name="psum_z", bufs=PER_BANK))
         psum_t = ctx.enter_context(tc.psum_pool(name="psum_t", bufs=PER_BANK))
 
-        sine_bf = tiny.tile([P, 1], BF16)
-        nc.sync.dma_start(out=sine_bf[:], in_=sine_w.partition_broadcast(P))
-        cosine_bf = tiny.tile([P, 1], BF16)
-        nc.sync.dma_start(out=cosine_bf[:], in_=cosine_w.partition_broadcast(P))
+        scalar_row = keep.tile([P, 4 * APART], BF16)
+        nc.vector.memset(scalar_row[:], 0.0)
+        for position, scalar in enumerate((sine_w, cosine_w, w, p)):
+            nc.sync.dma_start(
+                out=scalar_row[0:1, position * APART : position * APART + 1], in_=scalar.rearrange("(o n) -> o n", o=1)
+            )
+        ones = keep.tile([P, P], BF16)
+        nc.vector.memset(ones[:], 1.0)
         p_rows_bf = keep.tile([P, P], BF16)
         nc.vector.memset(p_rows_bf[:], 0.0)
         nc.scalar.dma_start(out=p_rows_bf[0:N_TILES, :], in_=P_vec.rearrange("(j n) -> j n", n=P))
@@ -62,16 +67,12 @@ def tile_time2vec_kernel(tc, x, W_words, W_scales, P_vec, w, p, sine_w, cosine_w
         x_sb = keep.tile([P, ROW_TILES, K_DIM], BF16)
         x_rows = x.rearrange("(i b) k -> i b k", b=P)
         w_words = keep.tile([P, PASSES, 2 * N_DIM], U8, align_bytes=64)
-        w_bf = tiny.tile([P, 1], BF16)
-        p_bf = tiny.tile([P, 1], BF16)
 
         for i in range(PER_BANK):
             nc.sync.dma_start(out=x_sb[:, i, :], in_=x_rows[i])
         for r in range(4):
             nc.sync.dma_start(out=w_scales[r:P:32, :, :].bitcast(I32), in_=scale_rows[r])
         nc.sync.dma_start(out=w_words[:].bitcast(I32), in_=W_words.bitcast(I32).rearrange("g p n -> p g n"))
-        nc.sync.dma_start(out=w_bf[:], in_=w.partition_broadcast(P))
-        nc.sync.dma_start(out=p_bf[:], in_=p.partition_broadcast(P))
         for i in range(PER_BANK, ROW_TILES):
             nc.sync.dma_start(out=x_sb[:, i, :], in_=x_rows[i])
 
@@ -181,21 +182,29 @@ def tile_time2vec_kernel(tc, x, W_words, W_scales, P_vec, w, p, sine_w, cosine_w
 
         def linear(i):
             original = leaving.tile([P, K_DIM], F32)
-            nc.vector.tensor_scalar(
-                out=original[:], in0=x_sb[:, i, :], scalar1=w32[:, 0:1], scalar2=p32[:, 0:1], op0=ALU.mult, op1=ALU.add
+            nc.gpsimd.tensor_scalar(
+                out=original[:], in0=x_sb[:, i, :], scalar1=w32, scalar2=p32, op0=ALU.mult, op1=ALU.add
             )
             nc.sync.dma_start(out=out[i * P : (i + 1) * P, 0:K_DIM], in_=original[:])
 
+        scalars_ps = psum_t.tile([P, 4 * APART], F32, tag="turned")
+        nc.tensor.matmul(out=scalars_ps[:], lhsT=ones[:], rhs=scalar_row[:], start=True, stop=True)
+        scalars = tiny.tile([P, 4 * APART], F32)
+        nc.vector.tensor_copy(out=scalars[:], in_=scalars_ps[:])
+        sine_32 = scalars[:, 0:1]
+        cosine_32 = scalars[:, APART : APART + 1]
+        w32 = scalars[:, 2 * APART : 2 * APART + 1]
+        p32 = scalars[:, 3 * APART : 3 * APART + 1]
         abs_sine = tiny.tile([P, 1], F32)
         nc.vector.scalar_tensor_tensor(
-            out=abs_sine[:], in0=sine_bf[:], scalar=-1.0, in1=sine_bf[:], op0=ALU.mult, op1=ALU.max
+            out=abs_sine[:], in0=sine_32, scalar=-1.0, in1=sine_32, op0=ALU.mult, op1=ALU.max
         )
         abs_cosine = tiny.tile([P, 1], F32)
         nc.vector.scalar_tensor_tensor(
-            out=abs_cosine[:], in0=cosine_bf[:], scalar=-1.0, in1=cosine_bf[:], op0=ALU.mult, op1=ALU.max
+            out=abs_cosine[:], in0=cosine_32, scalar=-1.0, in1=cosine_32, op0=ALU.mult, op1=ALU.max
         )
         twice = tiny.tile([P, 1], F32)
-        nc.vector.tensor_scalar(out=twice[:], in0=cosine_bf[:], scalar1=0.0, scalar2=2.0, op0=ALU.is_ge, op1=ALU.mult)
+        nc.vector.tensor_scalar(out=twice[:], in0=cosine_32, scalar1=0.0, scalar2=2.0, op0=ALU.is_ge, op1=ALU.mult)
         size = tiny.tile([P, 1], F32)
         nc.vector.scalar_tensor_tensor(
             out=size[:], in0=abs_cosine[:], scalar=TINY, in1=abs_sine[:], op0=ALU.max, op1=ALU.add
@@ -209,7 +218,7 @@ def tile_time2vec_kernel(tc, x, W_words, W_scales, P_vec, w, p, sine_w, cosine_w
         sign = tiny.tile([P, 1], F32)
         nc.vector.tensor_scalar(out=sign[:], in0=twice[:], scalar1=1.0, scalar2=None, op0=ALU.subtract)
         unit = tiny.tile([P, 2], F32)
-        nc.vector.tensor_tensor(out=unit[:, 0:1], in0=sine_bf[:], in1=inv_size[:], op=ALU.mult)
+        nc.vector.tensor_tensor(out=unit[:, 0:1], in0=sine_32, in1=inv_size[:], op=ALU.mult)
         abs_second = tiny.tile([P, 1], F32)
         nc.vector.scalar_tensor_tensor(
             out=abs_second[:], in0=abs_cosine[:], scalar=TINY, in1=inv_size[:], op0=ALU.max, op1=ALU.mult
@@ -291,10 +300,6 @@ def tile_time2vec_kernel(tc, x, W_words, W_scales, P_vec, w, p, sine_w, cosine_w
         )
         bias_rad = tiny.tile([P, N_TILES], F32)
         nc.gpsimd.tensor_scalar(out=bias_rad[:], in0=p_cols[:], scalar1=phase[:, 0:1], scalar2=None, op0=ALU.add)
-        w32 = tiny.tile([P, 1], F32)
-        nc.gpsimd.tensor_copy(out=w32[:], in_=w_bf[:])
-        p32 = tiny.tile([P, 1], F32)
-        nc.gpsimd.tensor_copy(out=p32[:], in_=p_bf[:])
 
         z_tiles = {}
         for slot in range(PER_BANK):

@@ -172,13 +172,32 @@ def tile_time2vec_kernel(tc, x, W_words, W_scales, P_vec, w, p, sine_w, cosine_w
 
         def leave(slot, back):
             half, group, c = place(slot)
-            periodic = leaving.tile([P, BANK], F32)
-            if slot >= SLOTS - PER_BANK and c % 2 == 1:
-                nc.vector.tensor_scalar(out=periodic[:], in0=back[:], scalar1=amp[:, 0:1], scalar2=None, op0=ALU.mult)
-            else:
-                nc.scalar.activation(out=periodic[:], in_=back[:], func=ACT.Copy, scale=amp[:, 0:1])
+            periodic = leaving.tile([P, BANK], F32, tag="periodic")
+            nc.scalar.activation(out=periodic[:], in_=back[:], func=ACT.Copy, scale=amp[:, 0:1])
             rows = slice((half * PER_BANK + c) * P, (half * PER_BANK + c + 1) * P)
             nc.sync.dma_start(out=out[rows, K_DIM + group * BANK : K_DIM + (group + 1) * BANK], in_=periodic[:])
+
+        def turn_slot(slot, wave):
+            half, group, position = place(slot)
+            back = psum_t.tile([P, PER_BANK, P], F32, tag="turned")
+            for c in range(PER_BANK):
+                nc.tensor.transpose(out=back[:, c, :], in_=wave[:, position, c * P : (c + 1) * P], identity=ident[:])
+            return back
+
+        def leave_slot(slot, back):
+            half, group, position = place(slot)
+            j = group * PER_BANK + position
+            strip = leaving.tile([P, PER_BANK, P], F32, tag="periodic")
+            if slot == SLOTS - 1:
+                nc.scalar.activation(out=strip[:], in_=back[:], func=ACT.Copy, scale=amp[:, 0:1])
+            else:
+                nc.vector.tensor_scalar(out=strip[:], in0=back[:], scalar1=amp[:, 0:1], scalar2=None, op0=ALU.mult)
+            nc.sync.dma_start(
+                out=out[half * BANK : (half + 1) * BANK, K_DIM + j * P : K_DIM + (j + 1) * P].rearrange(
+                    "(c b) n -> b c n", b=P
+                ),
+                in_=strip[:],
+            )
 
         def linear(i):
             original = leaving.tile([P, K_DIM], F32)
@@ -311,7 +330,8 @@ def tile_time2vec_kernel(tc, x, W_words, W_scales, P_vec, w, p, sine_w, cosine_w
         wholes = {0: nearest(0, z_tiles[0])}
         backs = {}
         wave = None
-        for slot in range(SLOTS + PER_BANK):
+        LAST = SLOTS - PER_BANK
+        for slot in range(SLOTS + 1):
             if slot + 1 < SLOTS:
                 wholes[slot + 1] = nearest(slot + 1, z_tiles[slot + 1])
             if slot < SLOTS:
@@ -322,12 +342,16 @@ def tile_time2vec_kernel(tc, x, W_words, W_scales, P_vec, w, p, sine_w, cosine_w
                 regroup(PER_BANK + slot, late_rows[PER_BANK + slot])
             if slot == ROW_TILES - PER_BANK:
                 quantise_half(1)
-            if slot >= PER_BANK:
+            if PER_BANK <= slot < SLOTS:
                 leave(slot - PER_BANK, backs[slot - PER_BANK])
+            if slot > LAST:
+                leave_slot(slot - 1, backs[slot - 1])
             if slot + PER_BANK < SLOTS:
                 z_tiles[slot + PER_BANK] = multiply(slot + PER_BANK)
             if slot < ROW_TILES:
                 linear(slot)
-            if slot < SLOTS and slot % PER_BANK == PER_BANK - 1:
+            if slot < LAST and slot % PER_BANK == PER_BANK - 1:
                 for c in range(PER_BANK):
                     backs[slot - (PER_BANK - 1) + c] = turn_back(c, wave)
+            if LAST <= slot < SLOTS:
+                backs[slot] = turn_slot(slot, wave)

@@ -26,10 +26,13 @@ HALVES = BATCH // BANK
 UNITS = HALVES * (N_TILES // PER_BANK)
 
 TWO_PI = 2.0 * math.pi
-HALF_PI = 0.5 * math.pi
+ATAN = (
+    0.9999999999293034, -0.3333333129088546, 0.1999990110203137, -0.14283813253845248,
+    0.11091922949633486, -0.08974171895628884, 0.07228278167635424, -0.05395667730662497,
+    0.033826215081032, -0.015828319890303207, 0.004732482998793988, -0.0006633952413764076,
+)
 APART = 16
 TINY = 1e-30
-SLOTS = UNITS * PER_BANK
 
 FLOPS = 2 * BATCH * K_DIM * N_DIM
 
@@ -45,41 +48,57 @@ def tile_time2vec_kernel(tc, x, W_words, W_scales, P_vec, w, p, sine_w, cosine_w
         psum_z = ctx.enter_context(tc.psum_pool(name="psum_z", bufs=PER_BANK))
         psum_t = ctx.enter_context(tc.psum_pool(name="psum_t", bufs=PER_BANK))
 
-        scalar_row = keep.tile([P, 4 * APART], BF16)
-        nc.vector.memset(scalar_row[:], 0.0)
-        for position, scalar in enumerate((sine_w, cosine_w, w, p)):
+        trig_row = keep.tile([P, 2 * APART], BF16)
+        nc.gpsimd.memset(trig_row[:], 0.0)
+        for position, scalar in enumerate((sine_w, cosine_w)):
             nc.sync.dma_start(
-                out=scalar_row[0:1, position * APART : position * APART + 1], in_=scalar.rearrange("(o n) -> o n", o=1)
+                out=trig_row[0:1, position * APART : position * APART + 1], in_=scalar.rearrange("(o n) -> o n", o=1)
             )
-        ones = keep.tile([P, P], BF16)
-        nc.vector.memset(ones[:], 1.0)
         p_rows_bf = keep.tile([P, P], BF16)
-        nc.vector.memset(p_rows_bf[:], 0.0)
+        nc.gpsimd.memset(p_rows_bf[:], 0.0)
         nc.scalar.dma_start(out=p_rows_bf[0:N_TILES, :], in_=P_vec.rearrange("(j n) -> j n", n=P))
         zero = tiny.tile([P, 1], F32)
-        nc.vector.memset(zero[:], 0.0)
+        nc.gpsimd.memset(zero[:], 0.0)
         warm = tiny.tile([P, 1], F32)
         nc.scalar.activation(out=warm[:], in_=zero[:], func=ACT.Sin)
-
-        w_scales = keep.tile([P, PASSES, N_DIM], U8, align_bytes=64)
-        nc.vector.memset(w_scales[:].bitcast(I32), 0)
-        scale_rows = W_scales.bitcast(I32).rearrange("g (quad r) n -> r quad g n", r=4)
-        x_sb = keep.tile([P, ROW_TILES, K_DIM], BF16)
-        x_rows = x.rearrange("(i b) k -> i b k", b=P)
-        w_words = keep.tile([P, PASSES, 2 * N_DIM], U8, align_bytes=64)
-
-        for i in range(PER_BANK):
-            nc.sync.dma_start(out=x_sb[:, i, :], in_=x_rows[i])
-        for r in range(4):
-            nc.sync.dma_start(out=w_scales[r:P:32, :, :].bitcast(I32), in_=scale_rows[r])
-        nc.sync.dma_start(out=w_words[:].bitcast(I32), in_=W_words.bitcast(I32).rearrange("g p n -> p g n"))
-        for i in range(PER_BANK, ROW_TILES):
-            nc.sync.dma_start(out=x_sb[:, i, :], in_=x_rows[i])
-
+        ones = keep.tile([P, P], BF16)
+        nc.vector.memset(ones[:], 1.0)
         ident = keep.tile([P, P], F32)
         make_identity(nc, ident[:])
         one_half = tiny.tile([P, 1], F32)
         nc.gpsimd.memset(one_half[:], 0.5)
+
+        x_sb = keep.tile([P, ROW_TILES, K_DIM], BF16)
+        x_rows = x.rearrange("(i b) k -> i b k", b=P)
+        w_scales = keep.tile([P, PASSES, N_DIM], U8, align_bytes=64)
+        nc.vector.memset(w_scales[:].bitcast(I32), 0)
+        scale_rows = W_scales.bitcast(I32).rearrange("g (quad r) n -> r quad g n", r=4)
+        w_words = keep.tile([P, PASSES, 2 * N_DIM], U8, align_bytes=64)
+        w_bytes = W_words.rearrange("g p n -> p g n")
+
+        def load_rows(i):
+            nc.sync.dma_start(out=x_sb[:, i, :], in_=x_rows[i])
+
+        def load_weights(group):
+            cols = slice(group * 2 * BANK, (group + 1) * 2 * BANK)
+            nc.sync.dma_start(out=w_words[:, :, cols].bitcast(I32), in_=w_bytes[:, :, cols].bitcast(I32))
+
+        load_rows(0)
+        load_rows(1)
+        for r in range(4):
+            nc.sync.dma_start(out=w_scales[r:P:32, :, :].bitcast(I32), in_=scale_rows[r])
+        load_weights(0)
+        load_rows(2)
+        load_rows(3)
+        load_weights(1)
+        line_row = keep.tile([P, 2 * APART], BF16)
+        nc.gpsimd.memset(line_row[:], 0.0)
+        for position, scalar in enumerate((w, p)):
+            nc.sync.dma_start(
+                out=line_row[0:1, position * APART : position * APART + 1], in_=scalar.rearrange("(o n) -> o n", o=1)
+            )
+        for i in range(PER_BANK, ROW_TILES):
+            load_rows(i)
 
         grouped = keep.tile([P, HALVES, PASSES, BANK, PACK], BF16, align_bytes=64)
         x_codes = keep.tile([P, HALVES, PASSES, BANK], U32, align_bytes=64)
@@ -118,49 +137,45 @@ def tile_time2vec_kernel(tc, x, W_words, W_scales, P_vec, w, p, sine_w, cosine_w
                 in_=grouped[:, half, :, :, :].rearrange("p g b t -> p (g b t)"),
             )
 
-        def place(slot):
-            unit_no, position = divmod(slot, PER_BANK)
-            half, group = divmod(unit_no, N_TILES // PER_BANK)
-            return half, group, position
-
-        def multiply(slot):
-            half, group, position = place(slot)
-            j = group * PER_BANK + position
-            z_t = psum_z.tile([P, BANK], F32)
-            for g in range(PASSES):
-                nc.tensor.matmul_mx(
-                    out=z_t[:],
-                    lhsT=w_words[:, g, 2 * P * j : 2 * P * (j + 1)].bitcast(FP4X4),
-                    lhsT_scale=w_scales[:, g, P * j : P * (j + 1)],
-                    rhs=x_codes[:, half, g, :].bitcast(FP8X4),
-                    rhs_scale=x_scales[:, half, g, :],
-                    start=(g == 0),
-                    stop=(g == PASSES - 1),
-                )
+        def multiply(piece):
+            half, j, lo, hi = piece
+            z_t = psum_z.tile([P, BANK], F32, tag="z_t")
+            step = BANK if hi - lo == BANK else P
+            for first in range(lo, hi, step):
+                for g in range(PASSES):
+                    nc.tensor.matmul_mx(
+                        out=z_t[:, first - lo : first - lo + step],
+                        lhsT=w_words[:, g, 2 * P * j : 2 * P * (j + 1)].bitcast(FP4X4),
+                        lhsT_scale=w_scales[:, g, P * j : P * (j + 1)],
+                        rhs=x_codes[:, half, g, first : first + step].bitcast(FP8X4),
+                        rhs_scale=x_scales[:, half, g, first : first + step],
+                        start=(g == 0),
+                        stop=(g == PASSES - 1),
+                    )
             return z_t
 
-        def nearest(slot, z_t):
-            half, group, position = place(slot)
-            j = group * PER_BANK + position
+        def nearest(piece, z_t):
+            half, j, lo, hi = piece
             whole = work.tile([P, BANK], I32)
             nc.vector.tensor_scalar(
-                out=whole[:], in0=z_t[:], scalar1=1.0 / TWO_PI, scalar2=bias_turns[:, j : j + 1],
-                op0=ALU.mult, op1=ALU.add,
+                out=whole[:, 0 : hi - lo], in0=z_t[:, 0 : hi - lo], scalar1=1.0 / TWO_PI,
+                scalar2=bias_turns[:, j : j + 1], op0=ALU.mult, op1=ALU.add,
             )
             return whole
 
-        def sine(slot, z_t, whole, wave):
-            half, group, position = place(slot)
-            j = group * PER_BANK + position
+        def sine(piece, z_t, whole, wave):
+            half, j, lo, hi = piece
             frac = work.tile([P, BANK], F32)
             nc.vector.scalar_tensor_tensor(
-                out=frac[:], in0=z_t[:], scalar=1.0 / TWO_PI, in1=whole[:], op0=ALU.mult, op1=ALU.subtract
+                out=frac[:, 0 : hi - lo], in0=z_t[:, 0 : hi - lo], scalar=1.0 / TWO_PI, in1=whole[:, 0 : hi - lo],
+                op0=ALU.mult, op1=ALU.subtract,
             )
             nc.scalar.activation(
-                out=wave[:, position, :], in_=frac[:], func=ACT.Sin, scale=TWO_PI, bias=bias_rad[:, j : j + 1]
+                out=wave[:, j % PER_BANK, lo:hi], in_=frac[:, 0 : hi - lo], func=ACT.Sin, scale=TWO_PI,
+                bias=bias_rad[:, j : j + 1],
             )
 
-        def turn_back(c, wave):
+        def turn_back(half, group, c, wave):
             back = psum_t.tile([P, BANK], F32, tag="turned")
             for position in range(PER_BANK):
                 nc.tensor.transpose(
@@ -168,36 +183,39 @@ def tile_time2vec_kernel(tc, x, W_words, W_scales, P_vec, w, p, sine_w, cosine_w
                     in_=wave[:, position, c * P : (c + 1) * P],
                     identity=ident[:],
                 )
-            return back
 
-        def leave(slot, back):
-            half, group, c = place(slot)
-            periodic = leaving.tile([P, BANK], F32, tag="periodic")
-            nc.scalar.activation(out=periodic[:], in_=back[:], func=ACT.Copy, scale=amp[:, 0:1])
-            rows = slice((half * PER_BANK + c) * P, (half * PER_BANK + c + 1) * P)
-            nc.sync.dma_start(out=out[rows, K_DIM + group * BANK : K_DIM + (group + 1) * BANK], in_=periodic[:])
+            def leave():
+                periodic = leaving.tile([P, BANK], F32, tag="periodic")
+                nc.scalar.activation(out=periodic[:], in_=back[:], func=ACT.Copy, scale=amp[:, 0:1])
+                rows = slice((half * PER_BANK + c) * P, (half * PER_BANK + c + 1) * P)
+                nc.sync.dma_start(out=out[rows, K_DIM + group * BANK : K_DIM + (group + 1) * BANK], in_=periodic[:])
 
-        def turn_slot(slot, wave):
-            half, group, position = place(slot)
+            return leave
+
+        def turn_piece(piece, wave, on_vector):
+            half, j, lo, hi = piece
             back = psum_t.tile([P, PER_BANK, P], F32, tag="turned")
             for c in range(PER_BANK):
-                nc.tensor.transpose(out=back[:, c, :], in_=wave[:, position, c * P : (c + 1) * P], identity=ident[:])
-            return back
+                nc.tensor.transpose(
+                    out=back[:, c, :], in_=wave[:, j % PER_BANK, c * P : (c + 1) * P], identity=ident[:]
+                )
 
-        def leave_slot(slot, back):
-            half, group, position = place(slot)
-            j = group * PER_BANK + position
-            strip = leaving.tile([P, PER_BANK, P], F32, tag="periodic")
-            if slot == SLOTS - 1:
-                nc.scalar.activation(out=strip[:], in_=back[:], func=ACT.Copy, scale=amp[:, 0:1])
-            else:
-                nc.vector.tensor_scalar(out=strip[:], in0=back[:], scalar1=amp[:, 0:1], scalar2=None, op0=ALU.mult)
-            nc.sync.dma_start(
-                out=out[half * BANK : (half + 1) * BANK, K_DIM + j * P : K_DIM + (j + 1) * P].rearrange(
-                    "(c b) n -> b c n", b=P
-                ),
-                in_=strip[:],
-            )
+            def leave():
+                strip = leaving.tile([P, PER_BANK, P], F32, tag="periodic")
+                if on_vector:
+                    nc.vector.tensor_scalar(
+                        out=strip[:], in0=back[:], scalar1=amp[:, 0:1], scalar2=None, op0=ALU.mult
+                    )
+                else:
+                    nc.scalar.activation(out=strip[:], in_=back[:], func=ACT.Copy, scale=amp[:, 0:1])
+                nc.sync.dma_start(
+                    out=out[half * BANK : (half + 1) * BANK, K_DIM + j * P : K_DIM + (j + 1) * P].rearrange(
+                        "(c b) n -> b c n", b=P
+                    ),
+                    in_=strip[:],
+                )
+
+            return leave
 
         def linear(i):
             original = leaving.tile([P, K_DIM], F32)
@@ -206,152 +224,158 @@ def tile_time2vec_kernel(tc, x, W_words, W_scales, P_vec, w, p, sine_w, cosine_w
             )
             nc.sync.dma_start(out=out[i * P : (i + 1) * P, 0:K_DIM], in_=original[:])
 
-        scalars_ps = psum_t.tile([P, 4 * APART], F32, tag="turned")
-        nc.tensor.matmul(out=scalars_ps[:], lhsT=ones[:], rhs=scalar_row[:], start=True, stop=True)
-        scalars = tiny.tile([P, 4 * APART], F32)
-        nc.vector.tensor_copy(out=scalars[:], in_=scalars_ps[:])
-        sine_32 = scalars[:, 0:1]
-        cosine_32 = scalars[:, APART : APART + 1]
-        w32 = scalars[:, 2 * APART : 2 * APART + 1]
-        p32 = scalars[:, 3 * APART : 3 * APART + 1]
-        abs_sine = tiny.tile([P, 1], F32)
+        trig_ps = psum_z.tile([P, 2 * APART], F32, tag="z_t")
+        nc.tensor.matmul(out=trig_ps[:], lhsT=ones[:], rhs=trig_row[:], start=True, stop=True)
+        trig = tiny.tile([P, 2 * APART], F32)
+        nc.vector.tensor_copy(out=trig[:], in_=trig_ps[:])
+        both = trig[:, 0 : 2 * APART : APART]
+        sizes = tiny.tile([P, 2], F32)
+        nc.vector.scalar_tensor_tensor(out=sizes[:], in0=both, scalar=-1.0, in1=both, op0=ALU.mult, op1=ALU.max)
+        halves = tiny.tile([P, 2], F32)
+        nc.vector.tensor_scalar(out=halves[:], in0=both, scalar1=0.0, scalar2=-0.5, op0=ALU.is_ge, op1=ALU.add)
+        larger = tiny.tile([P, 1], F32)
         nc.vector.scalar_tensor_tensor(
-            out=abs_sine[:], in0=sine_32, scalar=-1.0, in1=sine_32, op0=ALU.mult, op1=ALU.max
+            out=larger[:], in0=sizes[:, 0:1], scalar=TINY, in1=sizes[:, 1:2], op0=ALU.max, op1=ALU.max
         )
-        abs_cosine = tiny.tile([P, 1], F32)
+        smaller = tiny.tile([P, 1], F32)
+        nc.vector.tensor_tensor(out=smaller[:], in0=sizes[:, 0:1], in1=sizes[:, 1:2], op=ALU.min)
+        flat = tiny.tile([P, 1], F32)
+        nc.vector.tensor_tensor(out=flat[:], in0=sizes[:, 0:1], in1=sizes[:, 1:2], op=ALU.is_ge)
+        signs = tiny.tile([P, 1], F32)
+        nc.vector.tensor_tensor(out=signs[:], in0=halves[:, 0:1], in1=halves[:, 1:2], op=ALU.mult)
+        inv_larger = tiny.tile([P, 1], F32)
+        nc.vector.reciprocal(out=inv_larger[:], in_=larger[:])
+        turn8 = tiny.tile([P, 1], F32)
         nc.vector.scalar_tensor_tensor(
-            out=abs_cosine[:], in0=cosine_32, scalar=-1.0, in1=cosine_32, op0=ALU.mult, op1=ALU.max
+            out=turn8[:], in0=flat[:], scalar=0.5, in1=signs[:], op0=ALU.subtract, op1=ALU.mult
         )
-        twice = tiny.tile([P, 1], F32)
-        nc.vector.tensor_scalar(out=twice[:], in0=cosine_32, scalar1=0.0, scalar2=2.0, op0=ALU.is_ge, op1=ALU.mult)
-        size = tiny.tile([P, 1], F32)
+        t8th = tiny.tile([P, 1], F32)
         nc.vector.scalar_tensor_tensor(
-            out=size[:], in0=abs_cosine[:], scalar=TINY, in1=abs_sine[:], op0=ALU.max, op1=ALU.add
+            out=t8th[:], in0=smaller[:], scalar=inv_larger[:, 0:1], in1=turn8[:], op0=ALU.mult, op1=ALU.mult
         )
-        quarter = tiny.tile([P, 1], F32)
-        nc.vector.tensor_scalar(out=quarter[:], in0=twice[:], scalar1=1.0, scalar2=HALF_PI, op0=ALU.subtract, op1=ALU.mult)
-        inv_size = tiny.tile([P, 1], F32)
-        nc.vector.reciprocal(out=inv_size[:], in_=size[:])
-        neg_quarter = tiny.tile([P, 1], F32)
-        nc.vector.tensor_scalar(out=neg_quarter[:], in0=quarter[:], scalar1=-1.0, scalar2=None, op0=ALU.mult)
-        sign = tiny.tile([P, 1], F32)
-        nc.vector.tensor_scalar(out=sign[:], in0=twice[:], scalar1=1.0, scalar2=None, op0=ALU.subtract)
-        unit = tiny.tile([P, 2], F32)
-        nc.vector.tensor_tensor(out=unit[:, 0:1], in0=sine_32, in1=inv_size[:], op=ALU.mult)
-        abs_second = tiny.tile([P, 1], F32)
+        power2 = tiny.tile([P, 1], F32)
         nc.vector.scalar_tensor_tensor(
-            out=abs_second[:], in0=abs_cosine[:], scalar=TINY, in1=inv_size[:], op0=ALU.max, op1=ALU.mult
+            out=power2[:], in0=t8th[:], scalar=64.0, in1=t8th[:], op0=ALU.mult, op1=ALU.mult
         )
-        regroup(0, turn_rows(0))
-        angles = tiny.tile([P, 2], F32)
-        nc.vector.tensor_scalar(
-            out=angles[:, 0:1], in0=unit[:, 0:1], scalar1=neg_quarter[:, 0:1], scalar2=quarter[:, 0:1],
-            op0=ALU.mult, op1=ALU.add,
+        corner_a = tiny.tile([P, 1], F32)
+        nc.vector.tensor_tensor(out=corner_a[:], in0=halves[:, 0:1], in1=flat[:], op=ALU.mult)
+        corner_b = tiny.tile([P, 1], F32)
+        nc.vector.tensor_scalar(out=corner_b[:], in0=corner_a[:], scalar1=-1.0, scalar2=0.5, op0=ALU.mult, op1=ALU.add)
+        corner = tiny.tile([P, 1], F32)
+        nc.vector.scalar_tensor_tensor(
+            out=corner[:], in0=corner_b[:], scalar=TWO_PI, in1=halves[:, 1:2], op0=ALU.mult, op1=ALU.mult
         )
-        nc.vector.tensor_scalar(out=angles[:, 1:2], in0=unit[:, 0:1], scalar1=HALF_PI, scalar2=None, op0=ALU.mult)
-        sin_cos = tiny.tile([P, 2], F32)
-        nc.scalar.activation(out=sin_cos[:], in_=angles[:], func=ACT.Sin)
-        nc.vector.tensor_tensor(out=unit[:, 1:2], in0=abs_second[:], in1=sign[:], op=ALU.mult)
-        neg_first = tiny.tile([P, 1], F32)
-        nc.vector.tensor_scalar(out=neg_first[:], in0=unit[:, 0:1], scalar1=-1.0, scalar2=None, op0=ALU.mult)
+        t8th_turns = tiny.tile([P, 1], F32)
+        nc.vector.tensor_scalar(out=t8th_turns[:], in0=t8th[:], scalar1=1.0 / TWO_PI, scalar2=None, op0=ALU.mult)
         p_rows = keep.tile([P, P], F32)
         nc.gpsimd.tensor_copy(out=p_rows[:], in_=p_rows_bf[:])
-        squares = tiny.tile([P, 2], F32)
-        nc.gpsimd.tensor_tensor(out=squares[:], in0=unit[:], in1=unit[:], op=ALU.mult)
-        norm2 = tiny.tile([P, 1], F32)
-        nc.gpsimd.tensor_tensor(out=norm2[:], in0=squares[:, 0:1], in1=squares[:, 1:2], op=ALU.add)
-        norm = tiny.tile([P, 1], F32)
-        nc.gpsimd.tensor_tensor(out=norm[:], in0=norm2[:], in1=one_half[:], op=ALU.pow)
-        amp = tiny.tile([P, 1], F32)
-        nc.gpsimd.tensor_tensor(out=amp[:], in0=size[:], in1=norm[:], op=ALU.mult)
-
-        regroup(1, turn_rows(1))
-        p_turned = psum_t.tile([P, P], F32, tag="turned")
+        p_turned = psum_z.tile([P, P], F32, tag="z_t")
         nc.tensor.transpose(out=p_turned[:], in_=p_rows[:], identity=ident[:])
-        regroup(2, turn_rows(2))
-        regroup(3, turn_rows(3))
-
-        quantise_tile(0, 0)
-        quantise_tile(0, 1)
-        by_cos = tiny.tile([P, 2], F32)
-        nc.vector.tensor_scalar(out=by_cos[:], in0=unit[:], scalar1=sin_cos[:, 1:2], scalar2=None, op0=ALU.mult)
-        p_cols = tiny.tile([P, N_TILES], F32)
-        nc.vector.tensor_copy(out=p_cols[:], in_=p_turned[:, 0:N_TILES])
-        cross = tiny.tile([P, 1], F32)
-        nc.vector.scalar_tensor_tensor(
-            out=cross[:], in0=sin_cos[:, 0:1], scalar=neg_first[:, 0:1], in1=by_cos[:, 1:2], op0=ALU.mult, op1=ALU.add
-        )
-        dot = tiny.tile([P, 1], F32)
-        nc.vector.scalar_tensor_tensor(
-            out=dot[:], in0=sin_cos[:, 0:1], scalar=unit[:, 1:2], in1=by_cos[:, 0:1], op0=ALU.mult, op1=ALU.add
-        )
-        quantise_tile(1, 0)
-        inv_dot = tiny.tile([P, 1], F32)
-        nc.vector.reciprocal(out=inv_dot[:], in_=dot[:])
-        quantise_tile(1, 1)
-        slope = tiny.tile([P, 1], F32)
-        nc.vector.tensor_tensor(out=slope[:], in0=cross[:], in1=inv_dot[:], op=ALU.mult)
-        quantise_tile(2, 0)
-        slope2 = tiny.tile([P, 1], F32)
-        nc.vector.tensor_tensor(out=slope2[:], in0=slope[:], in1=slope[:], op=ALU.mult)
-        quantise_tile(2, 1)
-        low = tiny.tile([P, 1], F32)
-        nc.vector.tensor_scalar(out=low[:], in0=slope2[:], scalar1=-1.0 / 3.0, scalar2=1.0, op0=ALU.mult, op1=ALU.add)
-        high = tiny.tile([P, 1], F32)
+        base_rad = tiny.tile([P, N_TILES], F32)
         nc.vector.tensor_scalar(
-            out=high[:], in0=slope2[:], scalar1=-1.0 / 7.0, scalar2=1.0 / 5.0, op0=ALU.mult, op1=ALU.add
+            out=base_rad[:], in0=p_turned[:, 0:N_TILES], scalar1=corner[:, 0:1], scalar2=None, op0=ALU.add
         )
-        slope4 = tiny.tile([P, 1], F32)
-        nc.vector.tensor_tensor(out=slope4[:], in0=slope2[:], in1=slope2[:], op=ALU.mult)
-        quantise_tile(3, 0)
+        base_turns = tiny.tile([P, N_TILES], F32)
+        nc.vector.tensor_scalar(
+            out=base_turns[:], in0=p_turned[:, 0:N_TILES], scalar1=corner[:, 0:1], scalar2=1.0 / TWO_PI,
+            op0=ALU.add, op1=ALU.mult,
+        )
+        pairs = []
+        for i in range(6):
+            pair = tiny.tile([P, 1], F32, name="pair%d" % i)
+            nc.vector.tensor_scalar(
+                out=pair[:], in0=power2[:], scalar1=8.0 * ATAN[2 * i + 1], scalar2=8.0 * ATAN[2 * i],
+                op0=ALU.mult, op1=ALU.add,
+            )
+            pairs.append(pair)
+        power4 = tiny.tile([P, 1], F32)
+        nc.vector.tensor_tensor(out=power4[:], in0=power2[:], in1=power2[:], op=ALU.mult)
+        fours = []
+        for i in range(3):
+            four = tiny.tile([P, 1], F32, name="four%d" % i)
+            nc.vector.scalar_tensor_tensor(
+                out=four[:], in0=pairs[2 * i + 1][:], scalar=power4[:, 0:1], in1=pairs[2 * i][:],
+                op0=ALU.mult, op1=ALU.add,
+            )
+            fours.append(four)
+        power8 = tiny.tile([P, 1], F32)
+        nc.vector.tensor_tensor(out=power8[:], in0=power4[:], in1=power4[:], op=ALU.mult)
+        eight = tiny.tile([P, 1], F32)
+        nc.vector.scalar_tensor_tensor(
+            out=eight[:], in0=fours[1][:], scalar=power8[:, 0:1], in1=fours[0][:], op0=ALU.mult, op1=ALU.add
+        )
+        power16 = tiny.tile([P, 1], F32)
+        nc.vector.tensor_tensor(out=power16[:], in0=power8[:], in1=power8[:], op=ALU.mult)
         series = tiny.tile([P, 1], F32)
         nc.vector.scalar_tensor_tensor(
-            out=series[:], in0=high[:], scalar=slope4[:, 0:1], in1=low[:], op0=ALU.mult, op1=ALU.add
-        )
-        quantise_tile(3, 1)
-        phase = tiny.tile([P, 1], F32)
-        nc.vector.tensor_scalar(
-            out=phase[:], in0=series[:], scalar1=slope[:, 0:1], scalar2=angles[:, 0:1], op0=ALU.mult, op1=ALU.add
+            out=series[:], in0=fours[2][:], scalar=power16[:, 0:1], in1=eight[:], op0=ALU.mult, op1=ALU.add
         )
         bias_turns = tiny.tile([P, N_TILES], F32)
-        nc.vector.tensor_scalar(
-            out=bias_turns[:], in0=p_cols[:], scalar1=phase[:, 0:1], scalar2=1.0 / TWO_PI, op0=ALU.add, op1=ALU.mult
+        nc.vector.scalar_tensor_tensor(
+            out=bias_turns[:], in0=series[:, 0:1].to_broadcast([P, N_TILES]), scalar=t8th_turns[:, 0:1],
+            in1=base_turns[:], op0=ALU.mult, op1=ALU.add,
         )
         bias_rad = tiny.tile([P, N_TILES], F32)
-        nc.gpsimd.tensor_scalar(out=bias_rad[:], in0=p_cols[:], scalar1=phase[:, 0:1], scalar2=None, op0=ALU.add)
+        nc.vector.scalar_tensor_tensor(
+            out=bias_rad[:], in0=series[:, 0:1].to_broadcast([P, N_TILES]), scalar=t8th[:, 0:1],
+            in1=base_rad[:], op0=ALU.mult, op1=ALU.add,
+        )
+        grown = tiny.tile([P, 1], F32)
+        nc.gpsimd.tensor_scalar(out=grown[:], in0=power2[:], scalar1=1.0, scalar2=1.0, op0=ALU.mult, op1=ALU.add)
+        root = tiny.tile([P, 1], F32)
+        nc.gpsimd.tensor_tensor(out=root[:], in0=grown[:], in1=one_half[:], op=ALU.pow)
+        amp = tiny.tile([P, 1], F32)
+        nc.gpsimd.tensor_tensor(out=amp[:], in0=larger[:], in1=root[:], op=ALU.mult)
+        line_ps = psum_z.tile([P, 2 * APART], F32, tag="z_t")
+        nc.tensor.matmul(out=line_ps[:], lhsT=ones[:], rhs=line_row[:], start=True, stop=True)
+        line = tiny.tile([P, 2 * APART], F32)
+        nc.vector.tensor_copy(out=line[:], in_=line_ps[:])
+        w32 = line[:, 0:1]
+        p32 = line[:, APART : APART + 1]
+
+        for i in range(PER_BANK):
+            regroup(i, turn_rows(i))
+            quantise_tile(i, 0)
+            quantise_tile(i, 1)
+
+        part = BANK // 2
+        pieces = [(0, j, lo, lo + part) for lo in (0, part) for j in range(PER_BANK)]
+        pieces += [(0, j, 0, BANK) for j in range(PER_BANK, N_TILES)]
+        pieces += [(1, j, 0, BANK) for j in range(N_TILES)]
+        count = len(pieces)
+        last_unit = count - PER_BANK
 
         z_tiles = {}
-        for slot in range(PER_BANK):
-            z_tiles[slot] = multiply(slot)
-        late_rows = {}
+        for k in range(PER_BANK):
+            z_tiles[k] = multiply(pieces[k])
         for i in range(PER_BANK, ROW_TILES):
-            late_rows[i] = turn_rows(i)
+            regroup(i, turn_rows(i))
+        quantise_half(1)
 
-        wholes = {0: nearest(0, z_tiles[0])}
-        backs = {}
+        wholes = {0: nearest(pieces[0], z_tiles[0])}
+        leaves = {}
+        left = 0
         wave = None
-        LAST = SLOTS - PER_BANK
-        for slot in range(SLOTS + 1):
-            if slot + 1 < SLOTS:
-                wholes[slot + 1] = nearest(slot + 1, z_tiles[slot + 1])
-            if slot < SLOTS:
-                if slot % PER_BANK == 0:
-                    wave = waves.tile([P, PER_BANK, BANK], F32, name="wave")
-                sine(slot, z_tiles[slot], wholes[slot], wave)
-            if slot < ROW_TILES - PER_BANK:
-                regroup(PER_BANK + slot, late_rows[PER_BANK + slot])
-            if slot == ROW_TILES - PER_BANK:
-                quantise_half(1)
-            if PER_BANK <= slot < SLOTS:
-                leave(slot - PER_BANK, backs[slot - PER_BANK])
-            if slot > LAST:
-                leave_slot(slot - 1, backs[slot - 1])
-            if slot + PER_BANK < SLOTS:
-                z_tiles[slot + PER_BANK] = multiply(slot + PER_BANK)
-            if slot < ROW_TILES:
-                linear(slot)
-            if slot < LAST and slot % PER_BANK == PER_BANK - 1:
-                for c in range(PER_BANK):
-                    backs[slot - (PER_BANK - 1) + c] = turn_back(c, wave)
-            if LAST <= slot < SLOTS:
-                backs[slot] = turn_slot(slot, wave)
+        rows_done = 0
+        for k in range(count):
+            half, j, lo, hi = pieces[k]
+            if k + 1 < count:
+                wholes[k + 1] = nearest(pieces[k + 1], z_tiles[k + 1])
+            if j % PER_BANK == 0 and lo == 0:
+                wave = waves.tile([P, PER_BANK, BANK], F32, name="wave")
+            sine(pieces[k], z_tiles[k], wholes[k], wave)
+            if left < len(leaves):
+                leaves[left]()
+                left += 1
+            if k + PER_BANK < count:
+                z_tiles[k + PER_BANK] = multiply(pieces[k + PER_BANK])
+            if rows_done < ROW_TILES:
+                linear(rows_done)
+                rows_done += 1
+            if k >= last_unit:
+                leaves[len(leaves)] = turn_piece(pieces[k], wave, on_vector=(k < count - 1))
+            elif j % PER_BANK == PER_BANK - 1:
+                for c in range(lo // P, hi // P):
+                    leaves[len(leaves)] = turn_back(half, j // PER_BANK, c, wave)
+        for number in range(left, len(leaves)):
+            leaves[number]()

@@ -47,6 +47,7 @@ def tile_time2vec_kernel(tc, x, W_words, W_scales, P_vec, w, p, sine_w, cosine_w
         leaving = ctx.enter_context(tc.tile_pool(name="leaving", bufs=8))
         psum_z = ctx.enter_context(tc.psum_pool(name="psum_z", bufs=PER_BANK))
         psum_t = ctx.enter_context(tc.psum_pool(name="psum_t", bufs=PER_BANK))
+        ctx.enter_context(tc.manual_schedule(engines={mybir.EngineType.PE}))
 
         trig_row = keep.tile([P, 2 * APART], BF16)
         nc.gpsimd.memset(trig_row[:], 0.0)
@@ -326,13 +327,6 @@ def tile_time2vec_kernel(tc, x, W_words, W_scales, P_vec, w, p, sine_w, cosine_w
         nc.gpsimd.tensor_tensor(out=root[:], in0=grown[:], in1=one_half[:], op=ALU.pow)
         amp = tiny.tile([P, 1], F32)
         nc.gpsimd.tensor_tensor(out=amp[:], in0=larger[:], in1=root[:], op=ALU.mult)
-        line_ps = psum_z.tile([P, 2 * APART], F32, tag="z_t")
-        nc.tensor.matmul(out=line_ps[:], lhsT=ones[:], rhs=line_row[:], start=True, stop=True)
-        line = tiny.tile([P, 2 * APART], F32)
-        nc.vector.tensor_copy(out=line[:], in_=line_ps[:])
-        w32 = line[:, 0:1]
-        p32 = line[:, APART : APART + 1]
-
         for i in range(PER_BANK):
             regroup(i, turn_rows(i))
             quantise_tile(i, 0)
@@ -348,6 +342,12 @@ def tile_time2vec_kernel(tc, x, W_words, W_scales, P_vec, w, p, sine_w, cosine_w
         z_tiles = {}
         for k in range(PER_BANK):
             z_tiles[k] = multiply(pieces[k])
+        line_ps = psum_t.tile([P, 2 * APART], F32, tag="turned")
+        nc.tensor.matmul(out=line_ps[:], lhsT=ones[:], rhs=line_row[:], start=True, stop=True)
+        line = tiny.tile([P, 2 * APART], F32)
+        nc.vector.tensor_copy(out=line[:], in_=line_ps[:])
+        w32 = line[:, 0:1]
+        p32 = line[:, APART : APART + 1]
         for i in range(PER_BANK, ROW_TILES):
             regroup(i, turn_rows(i))
         quantise_half(1)

@@ -47,59 +47,58 @@ def tile_time2vec_kernel(tc, x, W_words, W_scales, P_vec, w, p, sine_w, cosine_w
         leaving = ctx.enter_context(tc.tile_pool(name="leaving", bufs=8))
         psum_z = ctx.enter_context(tc.psum_pool(name="psum_z", bufs=PER_BANK))
         psum_t = ctx.enter_context(tc.psum_pool(name="psum_t", bufs=PER_BANK))
+        with tc.manual_schedule(engines={mybir.EngineType.SP}):
+            trig_row = keep.tile([P, 2 * APART], BF16)
+            nc.gpsimd.memset(trig_row[:], 0.0)
+            for position, scalar in enumerate((sine_w, cosine_w)):
+                nc.sync.dma_start(
+                    out=trig_row[0:1, position * APART : position * APART + 1], in_=scalar.rearrange("(o n) -> o n", o=1)
+                )
+            p_rows_bf = keep.tile([P, P], BF16)
+            nc.gpsimd.memset(p_rows_bf[:], 0.0)
+            nc.scalar.dma_start(out=p_rows_bf[0:N_TILES, :], in_=P_vec.rearrange("(j n) -> j n", n=P))
+            zero = tiny.tile([P, 1], F32)
+            nc.gpsimd.memset(zero[:], 0.0)
+            warm = tiny.tile([P, 1], F32)
+            nc.scalar.activation(out=warm[:], in_=zero[:], func=ACT.Sin)
+            ones = keep.tile([P, P], BF16)
+            nc.vector.memset(ones[:], 1.0)
+            ident = keep.tile([P, P], F32)
+            make_identity(nc, ident[:])
+            one_half = tiny.tile([P, 1], F32)
+            nc.gpsimd.memset(one_half[:], 0.5)
+
+            x_sb = keep.tile([P, ROW_TILES, K_DIM], BF16)
+            x_rows = x.rearrange("(i b) k -> i b k", b=P)
+            w_scales = keep.tile([P, PASSES, N_DIM], U8, align_bytes=64)
+            nc.vector.memset(w_scales[:].bitcast(I32), 0)
+            scale_rows = W_scales.bitcast(I32).rearrange("g (quad r) n -> r quad g n", r=4)
+            w_words = keep.tile([P, PASSES, 2 * N_DIM], U8, align_bytes=64)
+            w_bytes = W_words.rearrange("g p n -> p g n")
+
+            def load_rows(i):
+                nc.sync.dma_start(out=x_sb[:, i, :], in_=x_rows[i])
+
+            def load_weights(group):
+                cols = slice(group * 2 * BANK, (group + 1) * 2 * BANK)
+                nc.sync.dma_start(out=w_words[:, :, cols].bitcast(I32), in_=w_bytes[:, :, cols].bitcast(I32))
+
+            for i in range(PER_BANK):
+                load_rows(i)
+            load_weights(0)
+            for r in range(4):
+                nc.sync.dma_start(out=w_scales[r:P:32, :, :].bitcast(I32), in_=scale_rows[r])
+            load_weights(1)
+            line_row = keep.tile([P, 2 * APART], BF16)
+            nc.gpsimd.memset(line_row[:], 0.0)
+            for position, scalar in enumerate((w, p)):
+                nc.sync.dma_start(
+                    out=line_row[0:1, position * APART : position * APART + 1], in_=scalar.rearrange("(o n) -> o n", o=1)
+                )
+            for i in range(PER_BANK, ROW_TILES):
+                load_rows(i)
+
         ctx.enter_context(tc.manual_schedule(engines={mybir.EngineType.PE}))
-
-        trig_row = keep.tile([P, 2 * APART], BF16)
-        nc.gpsimd.memset(trig_row[:], 0.0)
-        for position, scalar in enumerate((sine_w, cosine_w)):
-            nc.sync.dma_start(
-                out=trig_row[0:1, position * APART : position * APART + 1], in_=scalar.rearrange("(o n) -> o n", o=1)
-            )
-        p_rows_bf = keep.tile([P, P], BF16)
-        nc.gpsimd.memset(p_rows_bf[:], 0.0)
-        nc.scalar.dma_start(out=p_rows_bf[0:N_TILES, :], in_=P_vec.rearrange("(j n) -> j n", n=P))
-        zero = tiny.tile([P, 1], F32)
-        nc.gpsimd.memset(zero[:], 0.0)
-        warm = tiny.tile([P, 1], F32)
-        nc.scalar.activation(out=warm[:], in_=zero[:], func=ACT.Sin)
-        ones = keep.tile([P, P], BF16)
-        nc.vector.memset(ones[:], 1.0)
-        ident = keep.tile([P, P], F32)
-        make_identity(nc, ident[:])
-        one_half = tiny.tile([P, 1], F32)
-        nc.gpsimd.memset(one_half[:], 0.5)
-
-        x_sb = keep.tile([P, ROW_TILES, K_DIM], BF16)
-        x_rows = x.rearrange("(i b) k -> i b k", b=P)
-        w_scales = keep.tile([P, PASSES, N_DIM], U8, align_bytes=64)
-        nc.vector.memset(w_scales[:].bitcast(I32), 0)
-        scale_rows = W_scales.bitcast(I32).rearrange("g (quad r) n -> r quad g n", r=4)
-        w_words = keep.tile([P, PASSES, 2 * N_DIM], U8, align_bytes=64)
-        w_bytes = W_words.rearrange("g p n -> p g n")
-
-        def load_rows(i):
-            nc.sync.dma_start(out=x_sb[:, i, :], in_=x_rows[i])
-
-        def load_weights(group):
-            cols = slice(group * 2 * BANK, (group + 1) * 2 * BANK)
-            nc.sync.dma_start(out=w_words[:, :, cols].bitcast(I32), in_=w_bytes[:, :, cols].bitcast(I32))
-
-        load_rows(0)
-        load_rows(1)
-        for r in range(4):
-            nc.sync.dma_start(out=w_scales[r:P:32, :, :].bitcast(I32), in_=scale_rows[r])
-        load_weights(0)
-        load_rows(2)
-        load_rows(3)
-        load_weights(1)
-        line_row = keep.tile([P, 2 * APART], BF16)
-        nc.gpsimd.memset(line_row[:], 0.0)
-        for position, scalar in enumerate((w, p)):
-            nc.sync.dma_start(
-                out=line_row[0:1, position * APART : position * APART + 1], in_=scalar.rearrange("(o n) -> o n", o=1)
-            )
-        for i in range(PER_BANK, ROW_TILES):
-            load_rows(i)
 
         grouped = keep.tile([P, HALVES, PASSES, BANK, PACK], BF16, align_bytes=64)
         x_codes = keep.tile([P, HALVES, PASSES, BANK], U32, align_bytes=64)

@@ -48,6 +48,13 @@ def tile_time2vec_kernel(tc, x, W_words, W_scales, P_vec, w, p, sine_w, cosine_w
         psum_z = ctx.enter_context(tc.psum_pool(name="psum_z", bufs=PER_BANK))
         psum_t = ctx.enter_context(tc.psum_pool(name="psum_t", bufs=PER_BANK))
         with tc.manual_schedule(engines={mybir.EngineType.SP}):
+            x_sb = keep.tile([P, ROW_TILES, K_DIM], BF16)
+            x_rows = x.rearrange("(i b) k -> i b k", b=P)
+
+            def load_rows(i):
+                nc.sync.dma_start(out=x_sb[:, i, :], in_=x_rows[i])
+
+            load_rows(0)
             trig_row = keep.tile([P, 2 * APART], BF16)
             nc.gpsimd.memset(trig_row[:], 0.0)
             for position, scalar in enumerate((sine_w, cosine_w)):
@@ -68,22 +75,17 @@ def tile_time2vec_kernel(tc, x, W_words, W_scales, P_vec, w, p, sine_w, cosine_w
             one_half = tiny.tile([P, 1], F32)
             nc.gpsimd.memset(one_half[:], 0.5)
 
-            x_sb = keep.tile([P, ROW_TILES, K_DIM], BF16)
-            x_rows = x.rearrange("(i b) k -> i b k", b=P)
             w_scales = keep.tile([P, PASSES, N_DIM], U8, align_bytes=64)
             nc.vector.memset(w_scales[:].bitcast(I32), 0)
             scale_rows = W_scales.bitcast(I32).rearrange("g (quad r) n -> r quad g n", r=4)
             w_words = keep.tile([P, PASSES, 2 * N_DIM], U8, align_bytes=64)
             w_bytes = W_words.rearrange("g p n -> p g n")
 
-            def load_rows(i):
-                nc.sync.dma_start(out=x_sb[:, i, :], in_=x_rows[i])
-
             def load_weights(group):
                 cols = slice(group * 2 * BANK, (group + 1) * 2 * BANK)
                 nc.sync.dma_start(out=w_words[:, :, cols].bitcast(I32), in_=w_bytes[:, :, cols].bitcast(I32))
 
-            for i in range(PER_BANK):
+            for i in range(1, PER_BANK):
                 load_rows(i)
             load_weights(0)
             for r in range(4):
@@ -100,7 +102,10 @@ def tile_time2vec_kernel(tc, x, W_words, W_scales, P_vec, w, p, sine_w, cosine_w
 
         ctx.enter_context(tc.manual_schedule(engines={mybir.EngineType.PE}))
 
-        grouped = keep.tile([P, HALVES, PASSES, BANK, PACK], BF16, align_bytes=64)
+        grouped_rows = [
+            keep.tile([P, PASSES, P, PACK], BF16, align_bytes=64, name="grouped_row%d" % i) for i in range(PER_BANK)
+        ]
+        grouped_half = keep.tile([P, PASSES, BANK, PACK], BF16, align_bytes=64)
         x_codes = keep.tile([P, HALVES, PASSES, BANK], U32, align_bytes=64)
         x_scales = keep.tile([P, HALVES, PASSES, BANK], U8, align_bytes=64)
 
@@ -116,10 +121,8 @@ def tile_time2vec_kernel(tc, x, W_words, W_scales, P_vec, w, p, sine_w, cosine_w
 
         def regroup(i, turned):
             half, c = divmod(i, PER_BANK)
-            nc.scalar.copy(
-                out=grouped[:, half, :, c * P : (c + 1) * P, :].bitcast(F32),
-                in_=turned[:].rearrange("p g u b -> p g b u"),
-            )
+            into = grouped_half[:, :, c * P : (c + 1) * P, :] if half else grouped_rows[c][:]
+            nc.scalar.copy(out=into.bitcast(F32), in_=turned[:].rearrange("p g u b -> p g b u"))
 
         def quantise_tile(i, g):
             half, c = divmod(i, PER_BANK)
@@ -127,14 +130,14 @@ def tile_time2vec_kernel(tc, x, W_words, W_scales, P_vec, w, p, sine_w, cosine_w
             nc.vector.quantize_mx(
                 out=x_codes[:, half, g, cols].bitcast(FP8X4),
                 scales=x_scales[:, half, g, cols],
-                in_=grouped[:, half, g, cols, :].rearrange("p b t -> p (b t)"),
+                in_=grouped_rows[c][:, g, :, :].rearrange("p b t -> p (b t)"),
             )
 
         def quantise_half(half):
             nc.vector.quantize_mx(
                 out=x_codes[:, half, :, :].rearrange("p g b -> p (g b)").bitcast(FP8X4),
                 scales=x_scales[:, half, :, :].rearrange("p g b -> p (g b)"),
-                in_=grouped[:, half, :, :, :].rearrange("p g b t -> p (g b t)"),
+                in_=grouped_half[:].rearrange("p g b t -> p (g b t)"),
             )
 
         def multiply(piece):
@@ -224,8 +227,17 @@ def tile_time2vec_kernel(tc, x, W_words, W_scales, P_vec, w, p, sine_w, cosine_w
             )
             nc.sync.dma_start(out=out[i * P : (i + 1) * P, 0:K_DIM], in_=original[:])
 
+        nothing = tiny.tile([P, 1], F32)
+        nc.vector.memset(nothing[:], 0.0)
+        coefficients = tiny.tile([P, len(ATAN) - 1], F32)
+        for position, coefficient in enumerate(reversed(ATAN[:-1])):
+            nc.vector.tensor_scalar(
+                out=coefficients[:, position : position + 1], in0=nothing[:], scalar1=8.0 * coefficient, scalar2=None,
+                op0=ALU.add,
+            )
         trig_ps = psum_z.tile([P, 2 * APART], F32, tag="z_t")
         nc.tensor.matmul(out=trig_ps[:], lhsT=ones[:], rhs=trig_row[:], start=True, stop=True)
+        turned = [turn_rows(0)]
         trig = tiny.tile([P, 2 * APART], F32)
         nc.vector.tensor_copy(out=trig[:], in_=trig_ps[:])
         both = trig[:, 0 : 2 * APART : APART]
@@ -269,6 +281,7 @@ def tile_time2vec_kernel(tc, x, W_words, W_scales, P_vec, w, p, sine_w, cosine_w
         nc.vector.tensor_scalar(out=t8th_turns[:], in0=t8th[:], scalar1=1.0 / TWO_PI, scalar2=None, op0=ALU.mult)
         p_rows = keep.tile([P, P], F32)
         nc.gpsimd.tensor_copy(out=p_rows[:], in_=p_rows_bf[:])
+        turned.append(turn_rows(1))
         p_turned = psum_z.tile([P, P], F32, tag="z_t")
         nc.tensor.transpose(out=p_turned[:], in_=p_rows[:], identity=ident[:])
         base_rad = tiny.tile([P, N_TILES], F32)
@@ -280,44 +293,20 @@ def tile_time2vec_kernel(tc, x, W_words, W_scales, P_vec, w, p, sine_w, cosine_w
             out=base_turns[:], in0=p_turned[:, 0:N_TILES], scalar1=corner[:, 0:1], scalar2=1.0 / TWO_PI,
             op0=ALU.add, op1=ALU.mult,
         )
-        pairs = []
-        for i in range(6):
-            pair = tiny.tile([P, 1], F32, name="pair%d" % i)
-            nc.vector.tensor_scalar(
-                out=pair[:], in0=power2[:], scalar1=8.0 * ATAN[2 * i + 1], scalar2=8.0 * ATAN[2 * i],
-                op0=ALU.mult, op1=ALU.add,
-            )
-            pairs.append(pair)
-        power4 = tiny.tile([P, 1], F32)
-        nc.vector.tensor_tensor(out=power4[:], in0=power2[:], in1=power2[:], op=ALU.mult)
-        fours = []
-        for i in range(3):
-            four = tiny.tile([P, 1], F32, name="four%d" % i)
-            nc.vector.scalar_tensor_tensor(
-                out=four[:], in0=pairs[2 * i + 1][:], scalar=power4[:, 0:1], in1=pairs[2 * i][:],
-                op0=ALU.mult, op1=ALU.add,
-            )
-            fours.append(four)
-        power8 = tiny.tile([P, 1], F32)
-        nc.vector.tensor_tensor(out=power8[:], in0=power4[:], in1=power4[:], op=ALU.mult)
-        eight = tiny.tile([P, 1], F32)
-        nc.vector.scalar_tensor_tensor(
-            out=eight[:], in0=fours[1][:], scalar=power8[:, 0:1], in1=fours[0][:], op0=ALU.mult, op1=ALU.add
+        horner = tiny.tile([P, len(ATAN) - 1], F32)
+        nc.vector.tensor_tensor_scan(
+            out=horner[:], data0=power2[:, 0:1].to_broadcast([P, len(ATAN) - 1]), data1=coefficients[:],
+            initial=8.0 * ATAN[-1], op0=ALU.mult, op1=ALU.add,
         )
-        power16 = tiny.tile([P, 1], F32)
-        nc.vector.tensor_tensor(out=power16[:], in0=power8[:], in1=power8[:], op=ALU.mult)
-        series = tiny.tile([P, 1], F32)
-        nc.vector.scalar_tensor_tensor(
-            out=series[:], in0=fours[2][:], scalar=power16[:, 0:1], in1=eight[:], op0=ALU.mult, op1=ALU.add
-        )
+        series = horner[:, len(ATAN) - 2 : len(ATAN) - 1]
         bias_turns = tiny.tile([P, N_TILES], F32)
         nc.vector.scalar_tensor_tensor(
-            out=bias_turns[:], in0=series[:, 0:1].to_broadcast([P, N_TILES]), scalar=t8th_turns[:, 0:1],
+            out=bias_turns[:], in0=series.to_broadcast([P, N_TILES]), scalar=t8th_turns[:, 0:1],
             in1=base_turns[:], op0=ALU.mult, op1=ALU.add,
         )
         bias_rad = tiny.tile([P, N_TILES], F32)
         nc.vector.scalar_tensor_tensor(
-            out=bias_rad[:], in0=series[:, 0:1].to_broadcast([P, N_TILES]), scalar=t8th[:, 0:1],
+            out=bias_rad[:], in0=series.to_broadcast([P, N_TILES]), scalar=t8th[:, 0:1],
             in1=base_rad[:], op0=ALU.mult, op1=ALU.add,
         )
         grown = tiny.tile([P, 1], F32)
@@ -326,8 +315,10 @@ def tile_time2vec_kernel(tc, x, W_words, W_scales, P_vec, w, p, sine_w, cosine_w
         nc.gpsimd.tensor_tensor(out=root[:], in0=grown[:], in1=one_half[:], op=ALU.pow)
         amp = tiny.tile([P, 1], F32)
         nc.gpsimd.tensor_tensor(out=amp[:], in0=larger[:], in1=root[:], op=ALU.mult)
+        for i in range(2, PER_BANK):
+            turned.append(turn_rows(i))
         for i in range(PER_BANK):
-            regroup(i, turn_rows(i))
+            regroup(i, turned[i])
             quantise_tile(i, 0)
             quantise_tile(i, 1)
 
@@ -347,9 +338,9 @@ def tile_time2vec_kernel(tc, x, W_words, W_scales, P_vec, w, p, sine_w, cosine_w
         nc.vector.tensor_copy(out=line[:], in_=line_ps[:])
         w32 = line[:, 0:1]
         p32 = line[:, APART : APART + 1]
-        for i in range(PER_BANK, ROW_TILES):
+        middle = PER_BANK + PER_BANK // 2
+        for i in range(PER_BANK, middle):
             regroup(i, turn_rows(i))
-        quantise_half(1)
 
         wholes = {0: nearest(pieces[0], z_tiles[0])}
         leaves = {}
@@ -371,6 +362,11 @@ def tile_time2vec_kernel(tc, x, W_words, W_scales, P_vec, w, p, sine_w, cosine_w
             if rows_done < ROW_TILES:
                 linear(rows_done)
                 rows_done += 1
+            if k == PER_BANK - 1:
+                for i in range(middle, ROW_TILES):
+                    regroup(i, turn_rows(i))
+            if k == 2 * PER_BANK - 1:
+                quantise_half(1)
             if k >= last_unit:
                 leaves[len(leaves)] = turn_piece(pieces[k], wave, on_vector=(k < count - 1))
             elif j % PER_BANK == PER_BANK - 1:

@@ -68,7 +68,7 @@ def tile_time2vec_kernel(tc, x, W_words, W_scales, P_vec, w, p, sine_w, cosine_w
             nc.gpsimd.memset(zero[:], 0.0)
             warm = tiny.tile([P, 1], F32)
             nc.scalar.activation(out=warm[:], in_=zero[:], func=ACT.Sin)
-            ones = keep.tile([P, P], BF16)
+            ones = keep.tile([P, BANK], BF16)
             nc.vector.memset(ones[:], 1.0)
             ident = keep.tile([P, P], F32)
             make_identity(nc, ident[:])
@@ -235,8 +235,11 @@ def tile_time2vec_kernel(tc, x, W_words, W_scales, P_vec, w, p, sine_w, cosine_w
                 out=coefficients[:, position : position + 1], in0=nothing[:], scalar1=8.0 * coefficient, scalar2=None,
                 op0=ALU.add,
             )
+        idle_ps = psum_z.tile([P, BANK], F32, tag="z_t")
+        for dummy in range(3):
+            nc.tensor.matmul(out=idle_ps[:], lhsT=ones[:, 0:P], rhs=ones[:], start=True, stop=True)
         trig_ps = psum_z.tile([P, 2 * APART], F32, tag="z_t")
-        nc.tensor.matmul(out=trig_ps[:], lhsT=ones[:], rhs=trig_row[:], start=True, stop=True)
+        nc.tensor.matmul(out=trig_ps[:], lhsT=ones[:, 0:P], rhs=trig_row[:], start=True, stop=True)
         turned = [turn_rows(0)]
         trig = tiny.tile([P, 2 * APART], F32)
         nc.vector.tensor_copy(out=trig[:], in_=trig_ps[:])
@@ -333,7 +336,7 @@ def tile_time2vec_kernel(tc, x, W_words, W_scales, P_vec, w, p, sine_w, cosine_w
         for k in range(PER_BANK):
             z_tiles[k] = multiply(pieces[k])
         line_ps = psum_t.tile([P, 2 * APART], F32, tag="turned")
-        nc.tensor.matmul(out=line_ps[:], lhsT=ones[:], rhs=line_row[:], start=True, stop=True)
+        nc.tensor.matmul(out=line_ps[:], lhsT=ones[:, 0:P], rhs=line_row[:], start=True, stop=True)
         line = tiny.tile([P, 2 * APART], F32)
         nc.vector.tensor_copy(out=line[:], in_=line_ps[:])
         w32 = line[:, 0:1]

@@ -105,7 +105,9 @@ def tile_time2vec_kernel(tc, x, W_words, W_scales, P_vec, w, p, sine_w, cosine_w
         grouped_rows = [
             keep.tile([P, PASSES, P, PACK], BF16, align_bytes=64, name="grouped_row%d" % i) for i in range(PER_BANK)
         ]
-        grouped_half = keep.tile([P, PASSES, BANK, PACK], BF16, align_bytes=64)
+        grouped_pairs = [
+            keep.tile([P, PASSES, BANK // 2, PACK], BF16, align_bytes=64, name="grouped_pair%d" % i) for i in range(2)
+        ]
         x_codes = keep.tile([P, HALVES, PASSES, BANK], U32, align_bytes=64)
         x_scales = keep.tile([P, HALVES, PASSES, BANK], U8, align_bytes=64)
 
@@ -121,7 +123,8 @@ def tile_time2vec_kernel(tc, x, W_words, W_scales, P_vec, w, p, sine_w, cosine_w
 
         def regroup(i, turned):
             half, c = divmod(i, PER_BANK)
-            into = grouped_half[:, :, c * P : (c + 1) * P, :] if half else grouped_rows[c][:]
+            pair, place = divmod(c, 2)
+            into = grouped_pairs[pair][:, :, place * P : (place + 1) * P, :] if half else grouped_rows[c][:]
             nc.scalar.copy(out=into.bitcast(F32), in_=turned[:].rearrange("p g u b -> p g b u"))
 
         def quantise_tile(i, g):
@@ -133,12 +136,14 @@ def tile_time2vec_kernel(tc, x, W_words, W_scales, P_vec, w, p, sine_w, cosine_w
                 in_=grouped_rows[c][:, g, :, :].rearrange("p b t -> p (b t)"),
             )
 
-        def quantise_half(half):
-            nc.vector.quantize_mx(
-                out=x_codes[:, half, :, :].rearrange("p g b -> p (g b)").bitcast(FP8X4),
-                scales=x_scales[:, half, :, :].rearrange("p g b -> p (g b)"),
-                in_=grouped_half[:].rearrange("p g b t -> p (g b t)"),
-            )
+        def quantise_pair(pair):
+            cols = slice(pair * 2 * P, (pair + 1) * 2 * P)
+            for g in range(PASSES):
+                nc.vector.quantize_mx(
+                    out=x_codes[:, 1, g, cols].bitcast(FP8X4),
+                    scales=x_scales[:, 1, g, cols],
+                    in_=grouped_pairs[pair][:, g, :, :].rearrange("p b t -> p (b t)"),
+                )
 
         def multiply(piece):
             half, j, lo, hi = piece
@@ -344,6 +349,7 @@ def tile_time2vec_kernel(tc, x, W_words, W_scales, P_vec, w, p, sine_w, cosine_w
         middle = PER_BANK + PER_BANK // 2
         for i in range(PER_BANK, middle):
             regroup(i, turn_rows(i))
+        quantise_pair(0)
 
         wholes = {0: nearest(pieces[0], z_tiles[0])}
         leaves = {}
@@ -352,11 +358,13 @@ def tile_time2vec_kernel(tc, x, W_words, W_scales, P_vec, w, p, sine_w, cosine_w
         rows_done = 0
         for k in range(count):
             half, j, lo, hi = pieces[k]
-            if k + 1 < count:
+            if 0 < k < count - 1:
                 wholes[k + 1] = nearest(pieces[k + 1], z_tiles[k + 1])
             if j % PER_BANK == 0 and lo == 0:
                 wave = waves.tile([P, PER_BANK, BANK], F32, name="wave")
             sine(pieces[k], z_tiles[k], wholes[k], wave)
+            if k == 0:
+                wholes[1] = nearest(pieces[1], z_tiles[1])
             if left < len(leaves):
                 leaves[left]()
                 left += 1
@@ -368,8 +376,7 @@ def tile_time2vec_kernel(tc, x, W_words, W_scales, P_vec, w, p, sine_w, cosine_w
             if k == PER_BANK - 1:
                 for i in range(middle, ROW_TILES):
                     regroup(i, turn_rows(i))
-            if k == 2 * PER_BANK - 1:
-                quantise_half(1)
+                quantise_pair(1)
             if k >= last_unit:
                 leaves[len(leaves)] = turn_piece(pieces[k], wave, on_vector=(k < count - 1))
             elif j % PER_BANK == PER_BANK - 1:

@@ -78,12 +78,15 @@ def tile_time2vec_kernel(tc, x, W_words, W_scales, P_vec, w, p, sine_w, cosine_w
             w_scales = keep.tile([P, PASSES, N_DIM], U8, align_bytes=64)
             nc.vector.memset(w_scales[:].bitcast(I32), 0)
             scale_rows = W_scales.bitcast(I32).rearrange("g (quad r) n -> r quad g n", r=4)
-            w_words = keep.tile([P, PASSES, 2 * N_DIM], U8, align_bytes=64)
+            w_words = [
+                keep.tile([P, PASSES, 2 * BANK], U8, align_bytes=64, name="w_words%d" % group)
+                for group in range(N_TILES // PER_BANK)
+            ]
             w_bytes = W_words.rearrange("g p n -> p g n")
 
             def load_weights(group):
                 cols = slice(group * 2 * BANK, (group + 1) * 2 * BANK)
-                nc.sync.dma_start(out=w_words[:, :, cols].bitcast(I32), in_=w_bytes[:, :, cols].bitcast(I32))
+                nc.sync.dma_start(out=w_words[group][:].bitcast(I32), in_=w_bytes[:, :, cols].bitcast(I32))
 
             for i in range(1, PER_BANK):
                 load_rows(i)
@@ -147,13 +150,14 @@ def tile_time2vec_kernel(tc, x, W_words, W_scales, P_vec, w, p, sine_w, cosine_w
 
         def multiply(piece):
             half, j, lo, hi = piece
+            group, position = divmod(j, PER_BANK)
             z_t = psum_z.tile([P, BANK], F32, tag="z_t")
             step = BANK if hi - lo == BANK else P
             for first in range(lo, hi, step):
                 for g in range(PASSES):
                     nc.tensor.matmul_mx(
                         out=z_t[:, first - lo : first - lo + step],
-                        lhsT=w_words[:, g, 2 * P * j : 2 * P * (j + 1)].bitcast(FP4X4),
+                        lhsT=w_words[group][:, g, 2 * P * position : 2 * P * (position + 1)].bitcast(FP4X4),
                         lhsT_scale=w_scales[:, g, P * j : P * (j + 1)],
                         rhs=x_codes[:, half, g, first : first + step].bitcast(FP8X4),
                         rhs_scale=x_scales[:, half, g, first : first + step],

@@ -93,14 +93,17 @@ def tile_time2vec_kernel(tc, x, W_words, W_scales, P_vec, w, p, sine_w, cosine_w
             load_weights(0)
             for r in range(4):
                 nc.sync.dma_start(out=w_scales[r:P:32, :, :].bitcast(I32), in_=scale_rows[r])
-            load_weights(1)
             line_row = keep.tile([P, 2 * APART], BF16)
             nc.gpsimd.memset(line_row[:], 0.0)
             for position, scalar in enumerate((w, p)):
                 nc.sync.dma_start(
                     out=line_row[0:1, position * APART : position * APART + 1], in_=scalar.rearrange("(o n) -> o n", o=1)
                 )
-            for i in range(PER_BANK, ROW_TILES):
+            middle = PER_BANK + PER_BANK // 2
+            for i in range(PER_BANK, middle):
+                load_rows(i)
+            load_weights(1)
+            for i in range(middle, ROW_TILES):
                 load_rows(i)
 
         ctx.enter_context(tc.manual_schedule(engines={mybir.EngineType.PE}))
@@ -350,7 +353,6 @@ def tile_time2vec_kernel(tc, x, W_words, W_scales, P_vec, w, p, sine_w, cosine_w
         nc.vector.tensor_copy(out=line[:], in_=line_ps[:])
         w32 = line[:, 0:1]
         p32 = line[:, APART : APART + 1]
-        middle = PER_BANK + PER_BANK // 2
         for i in range(PER_BANK, middle):
             regroup(i, turn_rows(i))
         quantise_pair(0)

import math
from contextlib import ExitStack

import concourse.mybir as mybir
from concourse.masks import make_identity

F32 = mybir.dt.float32
BF16 = mybir.dt.bfloat16
I32 = mybir.dt.int32
U32 = mybir.dt.uint32
U8 = mybir.dt.uint8
FP8X4 = mybir.dt.float8_e4m3fn_x4
FP4X4 = mybir.dt.float4_e2m1fn_x4
ALU = mybir.AluOpType
ACT = mybir.ActivationFunctionType

P = 128
PACK = 4
BATCH, K_DIM, N_DIM = 1024, 1024, 1024
PASSES = K_DIM // (P * PACK)
BANK = 512
ROW_TILES = BATCH // P
N_TILES = N_DIM // P
PER_BANK = BANK // P
HALVES = BATCH // BANK
UNITS = HALVES * (N_TILES // PER_BANK)

TWO_PI = 2.0 * math.pi
ATAN = (
    0.9999999999293034, -0.3333333129088546, 0.1999990110203137, -0.14283813253845248,
    0.11091922949633486, -0.08974171895628884, 0.07228278167635424, -0.05395667730662497,
    0.033826215081032, -0.015828319890303207, 0.004732482998793988, -0.0006633952413764076,
)
APART = 16
TINY = 1e-30

FLOPS = 2 * BATCH * K_DIM * N_DIM


def tile_time2vec_kernel(tc, x, W_words, W_scales, P_vec, w, p, sine_w, cosine_w, out):
    nc = tc.nc
    with ExitStack() as ctx:
        keep = ctx.enter_context(tc.tile_pool(name="keep", bufs=1))
        tiny = ctx.enter_context(tc.tile_pool(name="tiny", bufs=1))
        work = ctx.enter_context(tc.tile_pool(name="work", bufs=4))
        waves = ctx.enter_context(tc.tile_pool(name="waves", bufs=2))
        leaving = ctx.enter_context(tc.tile_pool(name="leaving", bufs=8))
        psum_z = ctx.enter_context(tc.psum_pool(name="psum_z", bufs=PER_BANK))
        psum_t = ctx.enter_context(tc.psum_pool(name="psum_t", bufs=PER_BANK))
        with tc.manual_schedule(engines={mybir.EngineType.SP}):
            x_sb = keep.tile([P, ROW_TILES, K_DIM], BF16)
            x_rows = x.rearrange("(i b) k -> i b k", b=P)

            def load_rows(i):
                nc.sync.dma_start(out=x_sb[:, i, :], in_=x_rows[i])

            load_rows(0)
            trig_row = keep.tile([P, 2 * APART], BF16)
            nc.gpsimd.memset(trig_row[:], 0.0)
            for position, scalar in enumerate((sine_w, cosine_w)):
                nc.sync.dma_start(
                    out=trig_row[0:1, position * APART : position * APART + 1], in_=scalar.rearrange("(o n) -> o n", o=1)
                )
            p_rows_bf = keep.tile([P, P], BF16)
            nc.gpsimd.memset(p_rows_bf[:], 0.0)
            nc.scalar.dma_start(out=p_rows_bf[0:N_TILES, :], in_=P_vec.rearrange("(j n) -> j n", n=P))
            zero = tiny.tile([P, 1], F32)
            nc.gpsimd.memset(zero[:], 0.0)
            warm = tiny.tile([P, 1], F32)
            nc.scalar.activation(out=warm[:], in_=zero[:], func=ACT.Sin)
            ones = keep.tile([P, BANK], BF16)
            nc.vector.memset(ones[:], 1.0)
            ident = keep.tile([P, P], F32)
            make_identity(nc, ident[:])
            one_half = tiny.tile([P, 1], F32)
            nc.gpsimd.memset(one_half[:], 0.5)

            w_scales = keep.tile([P, PASSES, N_DIM], U8, align_bytes=64)
            nc.vector.memset(w_scales[:].bitcast(I32), 0)
            scale_rows = W_scales.bitcast(I32).rearrange("g (quad r) n -> r quad g n", r=4)
            w_words = [
                keep.tile([P, PASSES, 2 * BANK], U8, align_bytes=64, name="w_words%d" % group)
                for group in range(N_TILES // PER_BANK)
            ]
            w_bytes = W_words.rearrange("g p n -> p g n")

            def load_weights(group):
                cols = slice(group * 2 * BANK, (group + 1) * 2 * BANK)
                nc.sync.dma_start(out=w_words[group][:].bitcast(I32), in_=w_bytes[:, :, cols].bitcast(I32))

            for i in range(1, PER_BANK):
                load_rows(i)
            load_weights(0)
            for r in range(4):
                nc.sync.dma_start(out=w_scales[r:P:32, :, :].bitcast(I32), in_=scale_rows[r])
            line_row = keep.tile([P, 2 * APART], BF16)
            nc.gpsimd.memset(line_row[:], 0.0)
            for position, scalar in enumerate((w, p)):
                nc.sync.dma_start(
                    out=line_row[0:1, position * APART : position * APART + 1], in_=scalar.rearrange("(o n) -> o n", o=1)
                )
            middle = PER_BANK + PER_BANK // 2
            for i in range(PER_BANK, middle):
                load_rows(i)
            load_weights(1)
            for i in range(middle, ROW_TILES):
                load_rows(i)

        ctx.enter_context(tc.manual_schedule(engines={mybir.EngineType.PE}))

        grouped_rows = [
            keep.tile([P, PASSES, P, PACK], BF16, align_bytes=64, name="grouped_row%d" % i) for i in range(PER_BANK)
        ]
        grouped_pairs = [
            keep.tile([P, PASSES, BANK // 2, PACK], BF16, align_bytes=64, name="grouped_pair%d" % i) for i in range(2)
        ]
        x_codes = keep.tile([P, HALVES, PASSES, BANK], U32, align_bytes=64)
        x_scales = keep.tile([P, HALVES, PASSES, BANK], U8, align_bytes=64)

        def turn_rows(i):
            words = x_sb[:, i, :].bitcast(F32)
            turned = psum_t.tile([P, PASSES, 2, P], F32, tag="turned")
            for g in range(PASSES):
                for u in range(2):
                    nc.tensor.transpose(
                        out=turned[:, g, u, :], in_=words[:, 256 * g + u : 256 * (g + 1) : 2], identity=ident[:]
                    )
            return turned

        def regroup(i, turned):
            half, c = divmod(i, PER_BANK)
            pair, place = divmod(c, 2)
            into = grouped_pairs[pair][:, :, place * P : (place + 1) * P, :] if half else grouped_rows[c][:]
            nc.scalar.copy(out=into.bitcast(F32), in_=turned[:].rearrange("p g u b -> p g b u"))

        def quantise_tile(i, g):
            half, c = divmod(i, PER_BANK)
            cols = slice(c * P, (c + 1) * P)
            nc.vector.quantize_mx(
                out=x_codes[:, half, g, cols].bitcast(FP8X4),
                scales=x_scales[:, half, g, cols],
                in_=grouped_rows[c][:, g, :, :].rearrange("p b t -> p (b t)"),
            )

        def quantise_pair(pair):
            cols = slice(pair * 2 * P, (pair + 1) * 2 * P)
            for g in range(PASSES):
                nc.vector.quantize_mx(
                    out=x_codes[:, 1, g, cols].bitcast(FP8X4),
                    scales=x_scales[:, 1, g, cols],
                    in_=grouped_pairs[pair][:, g, :, :].rearrange("p b t -> p (b t)"),
                )

        def multiply(piece):
            half, j, lo, hi = piece
            group, position = divmod(j, PER_BANK)
            z_t = psum_z.tile([P, BANK], F32, tag="z_t")
            step = BANK if hi - lo == BANK else P
            for first in range(lo, hi, step):
                for g in range(PASSES):
                    nc.tensor.matmul_mx(
                        out=z_t[:, first - lo : first - lo + step],
                        lhsT=w_words[group][:, g, 2 * P * position : 2 * P * (position + 1)].bitcast(FP4X4),
                        lhsT_scale=w_scales[:, g, P * j : P * (j + 1)],
                        rhs=x_codes[:, half, g, first : first + step].bitcast(FP8X4),
                        rhs_scale=x_scales[:, half, g, first : first + step],
                        start=(g == 0),
                        stop=(g == PASSES - 1),
                    )
            return z_t

        def nearest(piece, z_t):
            half, j, lo, hi = piece
            whole = work.tile([P, BANK], I32)
            nc.vector.tensor_scalar(
                out=whole[:, 0 : hi - lo], in0=z_t[:, 0 : hi - lo], scalar1=1.0 / TWO_PI,
                scalar2=bias_turns[:, j : j + 1], op0=ALU.mult, op1=ALU.add,
            )
            return whole

        def sine(piece, z_t, whole, wave):
            half, j, lo, hi = piece
            frac = work.tile([P, BANK], F32)
            nc.vector.scalar_tensor_tensor(
                out=frac[:, 0 : hi - lo], in0=z_t[:, 0 : hi - lo], scalar=1.0 / TWO_PI, in1=whole[:, 0 : hi - lo],
                op0=ALU.mult, op1=ALU.subtract,
            )
            nc.scalar.activation(
                out=wave[:, j % PER_BANK, lo:hi], in_=frac[:, 0 : hi - lo], func=ACT.Sin, scale=TWO_PI,
                bias=bias_rad[:, j : j + 1],
            )

        def turn_back(half, group, c, wave):
            back = psum_t.tile([P, BANK], F32, tag="turned")
            for position in range(PER_BANK):
                nc.tensor.transpose(
                    out=back[:, position * P : (position + 1) * P],
                    in_=wave[:, position, c * P : (c + 1) * P],
                    identity=ident[:],
                )

            def leave():
                periodic = leaving.tile([P, BANK], F32, tag="periodic")
                nc.scalar.activation(out=periodic[:], in_=back[:], func=ACT.Copy, scale=amp[:, 0:1])
                rows = slice((half * PER_BANK + c) * P, (half * PER_BANK + c + 1) * P)
                nc.sync.dma_start(out=out[rows, K_DIM + group * BANK : K_DIM + (group + 1) * BANK], in_=periodic[:])

            return leave

        def turn_piece(piece, wave, on_vector):
            half, j, lo, hi = piece
            back = psum_t.tile([P, PER_BANK, P], F32, tag="turned")
            for c in range(PER_BANK):
                nc.tensor.transpose(
                    out=back[:, c, :], in_=wave[:, j % PER_BANK, c * P : (c + 1) * P], identity=ident[:]
                )

            def leave():
                strip = leaving.tile([P, PER_BANK, P], F32, tag="periodic")
                if on_vector:
                    nc.vector.tensor_scalar(
                        out=strip[:], in0=back[:], scalar1=amp[:, 0:1], scalar2=None, op0=ALU.mult
                    )
                else:
                    nc.scalar.activation(out=strip[:], in_=back[:], func=ACT.Copy, scale=amp[:, 0:1])
                nc.sync.dma_start(
                    out=out[half * BANK : (half + 1) * BANK, K_DIM + j * P : K_DIM + (j + 1) * P].rearrange(
                        "(c b) n -> b c n", b=P
                    ),
                    in_=strip[:],
                )

            return leave

        def linear(i):
            original = leaving.tile([P, K_DIM], F32)
            nc.gpsimd.tensor_scalar(
                out=original[:], in0=x_sb[:, i, :], scalar1=w32, scalar2=p32, op0=ALU.mult, op1=ALU.add
            )
            nc.sync.dma_start(out=out[i * P : (i + 1) * P, 0:K_DIM], in_=original[:])

        nothing = tiny.tile([P, 1], F32)
        nc.vector.memset(nothing[:], 0.0)
        coefficients = tiny.tile([P, len(ATAN) - 1], F32)
        for position, coefficient in enumerate(reversed(ATAN[:-1])):
            nc.vector.tensor_scalar(
                out=coefficients[:, position : position + 1], in0=nothing[:], scalar1=8.0 * coefficient, scalar2=None,
                op0=ALU.add,
            )
        idle_ps = psum_z.tile([P, BANK], F32, tag="z_t")
        for dummy in range(3):
            nc.tensor.matmul(out=idle_ps[:], lhsT=ones[:, 0:P], rhs=ones[:], start=True, stop=True)
        trig_ps = psum_z.tile([P, 2 * APART], F32, tag="z_t")
        nc.tensor.matmul(out=trig_ps[:], lhsT=ones[:, 0:P], rhs=trig_row[:], start=True, stop=True)
        turned = [turn_rows(0)]
        trig = tiny.tile([P, 2 * APART], F32)
        nc.vector.tensor_copy(out=trig[:], in_=trig_ps[:])
        both = trig[:, 0 : 2 * APART : APART]
        sizes = tiny.tile([P, 2], F32)
        nc.vector.scalar_tensor_tensor(out=sizes[:], in0=both, scalar=-1.0, in1=both, op0=ALU.mult, op1=ALU.max)
        halves = tiny.tile([P, 2], F32)
        nc.vector.tensor_scalar(out=halves[:], in0=both, scalar1=0.0, scalar2=-0.5, op0=ALU.is_ge, op1=ALU.add)
        larger = tiny.tile([P, 1], F32)
        nc.vector.scalar_tensor_tensor(
            out=larger[:], in0=sizes[:, 0:1], scalar=TINY, in1=sizes[:, 1:2], op0=ALU.max, op1=ALU.max
        )
        smaller = tiny.tile([P, 1], F32)
        nc.vector.tensor_tensor(out=smaller[:], in0=sizes[:, 0:1], in1=sizes[:, 1:2], op=ALU.min)
        flat = tiny.tile([P, 1], F32)
        nc.vector.tensor_tensor(out=flat[:], in0=sizes[:, 0:1], in1=sizes[:, 1:2], op=ALU.is_ge)
        signs = tiny.tile([P, 1], F32)
        nc.vector.tensor_tensor(out=signs[:], in0=halves[:, 0:1], in1=halves[:, 1:2], op=ALU.mult)
        inv_larger = tiny.tile([P, 1], F32)
        nc.vector.reciprocal(out=inv_larger[:], in_=larger[:])
        turn8 = tiny.tile([P, 1], F32)
        nc.vector.scalar_tensor_tensor(
            out=turn8[:], in0=flat[:], scalar=0.5, in1=signs[:], op0=ALU.subtract, op1=ALU.mult
        )
        t8th = tiny.tile([P, 1], F32)
        nc.vector.scalar_tensor_tensor(
            out=t8th[:], in0=smaller[:], scalar=inv_larger[:, 0:1], in1=turn8[:], op0=ALU.mult, op1=ALU.mult
        )
        power2 = tiny.tile([P, 1], F32)
        nc.vector.scalar_tensor_tensor(
            out=power2[:], in0=t8th[:], scalar=64.0, in1=t8th[:], op0=ALU.mult, op1=ALU.mult
        )
        corner_a = tiny.tile([P, 1], F32)
        nc.vector.tensor_tensor(out=corner_a[:], in0=halves[:, 0:1], in1=flat[:], op=ALU.mult)
        corner_b = tiny.tile([P, 1], F32)
        nc.vector.tensor_scalar(out=corner_b[:], in0=corner_a[:], scalar1=-1.0, scalar2=0.5, op0=ALU.mult, op1=ALU.add)
        corner = tiny.tile([P, 1], F32)
        nc.vector.scalar_tensor_tensor(
            out=corner[:], in0=corner_b[:], scalar=TWO_PI, in1=halves[:, 1:2], op0=ALU.mult, op1=ALU.mult
        )
        t8th_turns = tiny.tile([P, 1], F32)
        nc.vector.tensor_scalar(out=t8th_turns[:], in0=t8th[:], scalar1=1.0 / TWO_PI, scalar2=None, op0=ALU.mult)
        p_rows = keep.tile([P, P], F32)
        nc.gpsimd.tensor_copy(out=p_rows[:], in_=p_rows_bf[:])
        turned.append(turn_rows(1))
        p_turned = psum_z.tile([P, P], F32, tag="z_t")
        nc.tensor.transpose(out=p_turned[:], in_=p_rows[:], identity=ident[:])
        base_rad = tiny.tile([P, N_TILES], F32)
        nc.vector.tensor_scalar(
            out=base_rad[:], in0=p_turned[:, 0:N_TILES], scalar1=corner[:, 0:1], scalar2=None, op0=ALU.add
        )
        base_turns = tiny.tile([P, N_TILES], F32)
        nc.vector.tensor_scalar(
            out=base_turns[:], in0=p_turned[:, 0:N_TILES], scalar1=corner[:, 0:1], scalar2=1.0 / TWO_PI,
            op0=ALU.add, op1=ALU.mult,
        )
        horner = tiny.tile([P, len(ATAN) - 1], F32)
        nc.vector.tensor_tensor_scan(
            out=horner[:], data0=power2[:, 0:1].to_broadcast([P, len(ATAN) - 1]), data1=coefficients[:],
            initial=8.0 * ATAN[-1], op0=ALU.mult, op1=ALU.add,
        )
        series = horner[:, len(ATAN) - 2 : len(ATAN) - 1]
        bias_turns = tiny.tile([P, N_TILES], F32)
        nc.vector.scalar_tensor_tensor(
            out=bias_turns[:], in0=series.to_broadcast([P, N_TILES]), scalar=t8th_turns[:, 0:1],
            in1=base_turns[:], op0=ALU.mult, op1=ALU.add,
        )
        bias_rad = tiny.tile([P, N_TILES], F32)
        nc.vector.scalar_tensor_tensor(
            out=bias_rad[:], in0=series.to_broadcast([P, N_TILES]), scalar=t8th[:, 0:1],
            in1=base_rad[:], op0=ALU.mult, op1=ALU.add,
        )
        grown = tiny.tile([P, 1], F32)
        nc.gpsimd.tensor_scalar(out=grown[:], in0=power2[:], scalar1=1.0, scalar2=1.0, op0=ALU.mult, op1=ALU.add)
        root = tiny.tile([P, 1], F32)
        nc.gpsimd.tensor_tensor(out=root[:], in0=grown[:], in1=one_half[:], op=ALU.pow)
        amp = tiny.tile([P, 1], F32)
        nc.gpsimd.tensor_tensor(out=amp[:], in0=larger[:], in1=root[:], op=ALU.mult)
        for i in range(2, PER_BANK):
            turned.append(turn_rows(i))
        for i in range(PER_BANK):
            regroup(i, turned[i])
            quantise_tile(i, 0)
            quantise_tile(i, 1)

        part = BANK // 2
        pieces = [(0, j, lo, lo + part) for lo in (0, part) for j in range(PER_BANK)]
        pieces += [(0, j, 0, BANK) for j in range(PER_BANK, N_TILES)]
        pieces += [(1, j, 0, BANK) for j in range(N_TILES)]
        count = len(pieces)
        last_unit = count - PER_BANK

        z_tiles = {}
        for k in range(PER_BANK):
            z_tiles[k] = multiply(pieces[k])
        line_ps = psum_t.tile([P, 2 * APART], F32, tag="turned")
        nc.tensor.matmul(out=line_ps[:], lhsT=ones[:, 0:P], rhs=line_row[:], start=True, stop=True)
        line = tiny.tile([P, 2 * APART], F32)
        nc.vector.tensor_copy(out=line[:], in_=line_ps[:])
        w32 = line[:, 0:1]
        p32 = line[:, APART : APART + 1]
        for i in range(PER_BANK, middle):
            regroup(i, turn_rows(i))
        quantise_pair(0)

        wholes = {0: nearest(pieces[0], z_tiles[0])}
        leaves = {}
        left = 0
        wave = None
        rows_done = 0
        for k in range(count):
            half, j, lo, hi = pieces[k]
            if 0 < k < count - 1:
                wholes[k + 1] = nearest(pieces[k + 1], z_tiles[k + 1])
            if j % PER_BANK == 0 and lo == 0:
                wave = waves.tile([P, PER_BANK, BANK], F32, name="wave")
            sine(pieces[k], z_tiles[k], wholes[k], wave)
            if k == 0:
                wholes[1] = nearest(pieces[1], z_tiles[1])
            if left < len(leaves):
                leaves[left]()
                left += 1
            if k + PER_BANK < count:
                z_tiles[k + PER_BANK] = multiply(pieces[k + PER_BANK])
            if rows_done < ROW_TILES:
                linear(rows_done)
                rows_done += 1
            if k == PER_BANK - 1:
                for i in range(middle, ROW_TILES):
                    regroup(i, turn_rows(i))
                quantise_pair(1)
            if k >= last_unit:
                leaves[len(leaves)] = turn_piece(pieces[k], wave, on_vector=(k < count - 1))
            elif j % PER_BANK == PER_BANK - 1:
                for c in range(lo // P, hi // P):
                    leaves[len(leaves)] = turn_back(half, j // PER_BANK, c, wave)
        for number in range(left, len(leaves)):
            leaves[number]()
